import numpy as np
import ml_dtypes


def mxq(x, axis, fmt="e4m3"):
    dtype, down = {"e4m3": (ml_dtypes.float8_e4m3fn, 7), "e5m2": (ml_dtypes.float8_e5m2, 14)}[fmt]
    v = np.moveaxis(np.asarray(x, np.float32).astype(ml_dtypes.bfloat16).astype(np.float64), axis, -1)
    blocks = v.reshape(v.shape[:-1] + (-1, 32))
    amax = np.abs(blocks).max(-1, keepdims=True)
    byte = np.maximum(np.where(amax > 0, np.frexp(amax)[1] - 1 + 127, 0) - down, 1)
    scale = np.exp2(byte - 127.0)
    codes = (blocks / scale).astype(np.float32).astype(dtype).astype(np.float64)
    return np.moveaxis((codes * scale).reshape(v.shape), -1, axis)


WIDE = False


def mx_kscale(k):
    if not WIDE:
        return np.ones(k)
    levels = np.array([10, -10, 5, -5, 0])
    a = np.random.permutation(np.resize(levels, k // 512 * 4)).reshape(k // 512, 4)
    idx = np.arange(k)
    return np.exp2(a[idx // 512, idx % 128 // 32])


BF16 = ml_dtypes.bfloat16


def bf(x):
    return np.asarray(x, np.float32).astype(BF16)


def f64(x):
    return np.asarray(x).astype(np.float64)


B, N, R, F = 32, 8, 512, 1024
GAMMA = 10.0
STEP = 0.1
LOG2 = np.log(2.0)


def ssp(v):
    return np.maximum(v, 0.0) + np.log(1.0 + np.exp(-np.abs(v))) - LOG2


def setup_inputs():
    t = mx_kscale(F)
    t = t / t.min()
    return {"x": bf(np.random.standard_normal((B, N, F))),
            "distances": bf(np.random.uniform(0.0, STEP * R, (B, N, N))),
            "W1": bf(np.random.standard_normal((R, F)) * 0.5 * t[None, :]),
            "b1": bf(np.random.standard_normal(F) * 0.2 * t),
            "W2": bf(np.random.standard_normal((F, F)) * 2.0 / np.sqrt(F) / t[:, None]),
            "b2": bf(np.random.standard_normal(F) * 0.2)}


def reference(x, distances, W1, b1, W2, b2):
    centers = STEP * np.arange(R)
    e_k = np.exp(-GAMMA * (f64(distances)[..., None] - centers) ** 2)
    h = ssp((mxq(e_k, 3, "e4m3") @ mxq(f64(W1), 0, "e4m3")) + f64(b1))
    w_l = ssp((mxq(h, 3, "e4m3") @ mxq(f64(W2), 0, "e4m3")) + f64(b2))
    return np.sum(f64(x)[:, :, None, :] * w_l, axis=2)

@@ -1,0 +1,285 @@
+import math
+from contextlib import ExitStack
+
+import concourse.mybir as mybir
+from concourse.masks import make_identity
+
+F32 = mybir.dt.float32
+BF16 = mybir.dt.bfloat16
+U32 = mybir.dt.uint32
+U8 = mybir.dt.uint8
+FP8X4 = mybir.dt.float8_e4m3fn_x4
+ACT = mybir.ActivationFunctionType
+ALU = mybir.AluOpType
+AXIS = mybir.AxisListType
+
+P = 128
+PACK = 4
+TOKENS = 32 * 8 * 8
+ATOMS = 8
+BASIS = 512
+FEATURES = 1024
+FEATURE_TILES = FEATURES // P
+BANK = 512
+BLOCK = 128
+CHUNK = 512
+CHUNKS = TOKENS // CHUNK
+BANKS_PER_CHUNK = CHUNK // BANK
+GROUP = 4
+SIG_BANKS = 4
+FIN_BANKS = 4
+LN2 = math.log(2.0)
+LOG_FLOOR = 2.0 ** -60
+
+FLOPS = 2 * TOKENS * BASIS * FEATURES + 2 * TOKENS * FEATURES * FEATURES
+
+
+def tile_cfconv_pa_kernel(tc, x, distances, W1, b1, W2, b2, out):
+    nc = tc.nc
+    with ExitStack() as ctx:
+        ctx.enter_context(tc.manual_schedule())
+        keep = ctx.enter_context(tc.tile_pool(name="keep", bufs=1))
+        stage = ctx.enter_context(tc.tile_pool(name="stage", bufs=2))
+        sig_pool = ctx.enter_context(tc.tile_pool(name="sig_pool", bufs=6))
+        work = ctx.enter_context(tc.tile_pool(name="work", bufs=2))
+        psum_sig = ctx.enter_context(tc.psum_pool(name="psum_sig", bufs=SIG_BANKS))
+        psum_fin = ctx.enter_context(tc.psum_pool(name="psum_fin", bufs=FIN_BANKS))
+
+        dist_rows = keep.tile([P, TOKENS], BF16)
+        nc.vector.memset(dist_rows[:], 0.0)
+        nc.vector.memset(dist_rows[32:33, :], 1.0)
+        nc.vector.memset(dist_rows[64:65, :], 1.0)
+        nc.sync.dma_start(out=dist_rows[0:1, :], in_=distances.rearrange("(o b) i j -> o (b i j)", o=1))
+
+        w1_raw = keep.tile([P, PACK, FEATURES], BF16)
+        nc.sync.dma_start(out=w1_raw[:], in_=W1.rearrange("(p j) f -> p j f", j=PACK))
+        w2_raw = keep.tile([P, 2, PACK, FEATURES], BF16)
+        for g in range(2):
+            nc.sync.dma_start(
+                out=w2_raw[:, g, :, :],
+                in_=W2[g * BASIS : (g + 1) * BASIS, :].rearrange("(p t) n -> p t n", t=PACK),
+            )
+        b1_bf = keep.tile([P, FEATURE_TILES], BF16)
+        b2_bf = keep.tile([P, FEATURE_TILES], BF16)
+        x_sb = keep.tile([P, 2, FEATURES], BF16)
+        with nc.allow_non_contiguous_dma(reason="two small bias vectors, one value a partition and tile"):
+            nc.sync.dma_start(
+                out=b1_bf[:].rearrange("p (g t) -> p g t", t=PACK),
+                in_=b1.rearrange("(g p t) -> p g t", p=P, t=PACK),
+            )
+            nc.sync.dma_start(out=b2_bf[:], in_=b2.rearrange("(c p) -> p c", p=P))
+        nc.sync.dma_start(out=x_sb[:], in_=x.rearrange("(h b) i f -> (b i) h f", h=2))
+
+        centre_rows = keep.tile([P, PACK, P], BF16)
+        nc.gpsimd.memset(centre_rows[:], 0.0)
+        nc.gpsimd.memset(centre_rows[0:1, :, :], 10.0)
+        nc.gpsimd.iota(
+            centre_rows[32:33, :, :], pattern=[[0, PACK], [-PACK, P]], base=0, channel_multiplier=0,
+            allow_small_or_imprecise_dtypes=True,
+        )
+        nc.gpsimd.iota(
+            centre_rows[64:65, :, :], pattern=[[-1, PACK], [0, P]], base=0, channel_multiplier=0,
+            allow_small_or_imprecise_dtypes=True,
+        )
+        identity = keep.tile([P, P], F32)
+        make_identity(nc, identity[:])
+        log_floor = keep.tile([P, 1], F32)
+        nc.vector.memset(log_floor[:], LOG_FLOOR)
+
+        w1_codes = keep.tile([P, FEATURES], U32, align_bytes=64)
+        w1_scales = keep.tile([P, FEATURES], U8, align_bytes=64)
+        w2_codes = keep.tile([P, 2, FEATURES], U32, align_bytes=64)
+        w2_scales = keep.tile([P, 2, FEATURES], U8, align_bytes=64)
+        for g in range(2):
+            cols = slice(g * BANK, (g + 1) * BANK)
+            grouped = stage.tile([P, PACK, P, PACK], BF16, align_bytes=64, tag="grouped", name="grouped")
+            nc.vector.tensor_scalar(
+                out=grouped[:], in0=w1_raw[:, :, cols].rearrange("p j (m t) -> p t m j", t=PACK),
+                scalar1=-1.0, scalar2=None, op0=ALU.mult,
+            )
+            nc.vector.quantize_mx(
+                out=w1_codes[:, cols].bitcast(FP8X4), scales=w1_scales[:, cols],
+                in_=grouped[:].rearrange("p t m j -> p (t m j)"),
+            )
+        for g in range(2):
+            for half in range(2):
+                cols = slice(half * BANK, (half + 1) * BANK)
+                grouped = stage.tile([P, BANK, PACK], BF16, align_bytes=64, tag="grouped", name="grouped")
+                nc.vector.tensor_scalar(
+                    out=grouped[:], in0=w2_raw[:, g, :, cols].rearrange("p t n -> p n t"),
+                    scalar1=-1.0, scalar2=None, op0=ALU.mult,
+                )
+                nc.vector.quantize_mx(
+                    out=w2_codes[:, g, cols].bitcast(FP8X4), scales=w2_scales[:, g, cols],
+                    in_=grouped[:].rearrange("p n t -> p (n t)"),
+                )
+
+        neg_bias = {}
+        shift_bias = {}
+        for layer, bias_bf in ((1, b1_bf), (2, b2_bf)):
+            neg_bias[layer] = keep.tile([P, FEATURE_TILES], F32, name="neg_bias%d" % layer)
+            shift_bias[layer] = keep.tile([P, FEATURE_TILES], F32, name="shift_bias%d" % layer)
+            nc.vector.tensor_scalar(
+                out=neg_bias[layer][:], in0=bias_bf[:], scalar1=-1.0, scalar2=None, op0=ALU.mult
+            )
+            nc.vector.tensor_scalar(
+                out=shift_bias[layer][:], in0=bias_bf[:], scalar1=-1.0, scalar2=LN2, op0=ALU.mult, op1=ALU.add
+            )
+
+        e_bf = keep.tile([P, TOKENS, PACK], BF16, align_bytes=64)
+        e_codes = keep.tile([P, TOKENS], U32, align_bytes=64)
+        e_scales = keep.tile([P, TOKENS], U8, align_bytes=64)
+        for tb in range(TOKENS // BANK):
+            squares = stage.tile([P, BANK // BLOCK, BLOCK, PACK], F32)
+            for blk in range(BANK // BLOCK):
+                first = tb * BANK + blk * BLOCK
+                z = psum_sig.tile([P, PACK, BLOCK], F32, tag="sig", name="z")
+                for j in range(PACK):
+                    nc.tensor.matmul(
+                        out=z[:, j, :], lhsT=centre_rows[:, j, :], rhs=dist_rows[:, first : first + BLOCK],
+                        start=True, stop=True,
+                    )
+                nc.scalar.activation(
+                    out=squares[:, blk, :, :], in_=z[:].rearrange("p j w -> p w j"), func=ACT.Square
+                )
+            tokens = slice(tb * BANK, (tb + 1) * BANK)
+            nc.scalar.activation(
+                out=e_bf[:, tokens, :].rearrange("p w j -> p (w j)"),
+                in_=squares[:].rearrange("p b w j -> p (b w j)"),
+                func=ACT.Exp,
+                scale=-0.1,
+            )
+            nc.vector.quantize_mx(
+                out=e_codes[:, tokens].bitcast(FP8X4),
+                scales=e_scales[:, tokens],
+                in_=e_bf[:, tokens, :].rearrange("p w j -> p (w j)"),
+            )
+
+        h_codes = keep.tile([P, 2, TOKENS], U32, align_bytes=64)
+        h_scales = keep.tile([P, 2, TOKENS], U8, align_bytes=64)
+        neg_sums = keep.tile([P, FEATURE_TILES, TOKENS // ATOMS], F32)
+        out_rows = out.rearrange("b i f -> (b i) f")
+        sig_tiles = {}
+        neg_h_tiles = {}
+
+        def product(layer, tb, ft, pool, tag):
+            tokens = slice(tb * BANK, (tb + 1) * BANK)
+            cols = slice(ft * P, (ft + 1) * P)
+            acc = pool.tile([P, BANK], F32, tag=tag, name="acc")
+            if layer == 1:
+                nc.tensor.matmul_mx(
+                    out=acc[:],
+                    lhsT=w1_codes[:, cols].bitcast(FP8X4), lhsT_scale=w1_scales[:, cols],
+                    rhs=e_codes[:, tokens].bitcast(FP8X4), rhs_scale=e_scales[:, tokens],
+                    start=True, stop=True,
+                )
+            else:
+                for g in range(2):
+                    nc.tensor.matmul_mx(
+                        out=acc[:],
+                        lhsT=w2_codes[:, g, cols].bitcast(FP8X4), lhsT_scale=w2_scales[:, g, cols],
+                        rhs=h_codes[:, g, tokens].bitcast(FP8X4), rhs_scale=h_scales[:, g, tokens],
+                        start=(g == 0), stop=(g == 1),
+                    )
+            return acc
+
+        def sigmoid(unit):
+            layer, tb, ft = unit
+            group, i = divmod(ft, GROUP)
+            if i == 0:
+                sig_tiles[(layer, tb, group)] = sig_pool.tile([P, GROUP, BANK], F32, tag="sig_tile", name="sig_tile")
+            acc = product(layer, tb, ft, psum_sig, "sig")
+            nc.scalar.activation(
+                out=sig_tiles[(layer, tb, group)][:, i, :], in_=acc[:], func=ACT.Sigmoid,
+                bias=neg_bias[layer][:, ft : ft + 1],
+            )
+
+        def logarithm(layer, tb, group):
+            flat = sig_tiles[(layer, tb, group)][:].rearrange("p i w -> p (i w)")
+            nc.scalar.activation(out=flat, in_=flat, func=ACT.Ln, scale=2.0, bias=log_floor[:, 0:1])
+
+        def finish(unit):
+            layer, tb, ft = unit
+            group, i = divmod(ft, GROUP)
+            neg_log = sig_tiles[(layer, tb, group)][:, i, :]
+            tokens = slice(tb * BANK, (tb + 1) * BANK)
+            acc = product(layer, tb, ft, psum_fin, "fin")
+            if layer == 1:
+                if i == 0:
+                    neg_h_tiles[(tb, group)] = work.tile([P, GROUP, BANK], BF16, tag="neg_h", name="neg_h")
+                neg_h = neg_h_tiles[(tb, group)]
+                nc.vector.scalar_tensor_tensor(
+                    out=neg_h[:, i, :], in0=acc[:], scalar=shift_bias[1][:, ft : ft + 1], in1=neg_log,
+                    op0=ALU.add, op1=ALU.min,
+                )
+                if i == GROUP - 1:
+                    h_grouped = work.tile([P, BANK, PACK], BF16, align_bytes=64, tag="h_grouped", name="h_grouped")
+                    nc.vector.tensor_scalar(
+                        out=h_grouped[:], in0=neg_h[:].rearrange("p t w -> p w t"),
+                        scalar1=-1.0, scalar2=None, op0=ALU.mult,
+                    )
+                    nc.vector.quantize_mx(
+                        out=h_codes[:, group, tokens].bitcast(FP8X4),
+                        scales=h_scales[:, group, tokens],
+                        in_=h_grouped[:].rearrange("p w t -> p (w t)"),
+                    )
+            else:
+                neg_w = work.tile([P, BANK], F32, tag="neg_w", name="neg_w", bufs=3)
+                nc.vector.scalar_tensor_tensor(
+                    out=neg_w[:], in0=acc[:], scalar=shift_bias[2][:, ft : ft + 1], in1=neg_log,
+                    op0=ALU.add, op1=ALU.min,
+                )
+                pairs = BANK // ATOMS
+                nc.vector.tensor_reduce(
+                    out=neg_sums[:, ft, tb * pairs : (tb + 1) * pairs],
+                    in_=neg_w[:].rearrange("p (a j) -> p a j", j=ATOMS),
+                    axis=AXIS.X, op=ALU.add,
+                )
+
+        def store(half):
+            rows = slice(half * P, (half + 1) * P)
+            for group in range(FEATURE_TILES // GROUP):
+                turned = psum_fin.tile([P, GROUP, P], F32, tag="fin", name="turned")
+                for i in range(GROUP):
+                    nc.tensor.transpose(turned[:, i, :], neg_sums[:, group * GROUP + i, rows], identity[:])
+                cols = slice(group * BANK, (group + 1) * BANK)
+                result = work.tile([P, BANK], F32, tag="result", name="result")
+                nc.vector.scalar_tensor_tensor(
+                    out=result[:], in0=turned[:].rearrange("p i m -> p (i m)"), scalar=-1.0,
+                    in1=x_sb[:, half, cols], op0=ALU.mult, op1=ALU.mult,
+                )
+                nc.sync.dma_start(out=out_rows[rows, cols], in_=result[:])
+
+        def units(layer, chunk):
+            if chunk < 0 or chunk >= CHUNKS:
+                return []
+            banks = range(chunk * BANKS_PER_CHUNK, (chunk + 1) * BANKS_PER_CHUNK)
+            return [(layer, tb, ft) for tb in banks for ft in range(FEATURE_TILES)]
+
+        tokens_per_half = P * ATOMS
+        for unit in units(1, 0):
+            sigmoid(unit)
+        for r in range(CHUNKS + 1):
+            first = units(1, r)
+            second = units(2, r - 1)
+            following = units(1, r + 1) + units(2, r)
+            for layer, tb, ft in first + second:
+                if ft % GROUP == 0:
+                    logarithm(layer, tb, ft // GROUP)
+            for unit in first:
+                finish(unit)
+            done = (r - 1) * CHUNK
+            if done > 0 and done % tokens_per_half == 0:
+                store(done // tokens_per_half - 1)
+            for unit in second[:FIN_BANKS]:
+                finish(unit)
+            rest = second[FIN_BANKS:]
+            runs = len(following) // SIG_BANKS
+            for k in range(runs):
+                for later in following[k * SIG_BANKS : (k + 1) * SIG_BANKS]:
+                    sigmoid(later)
+                for unit in rest[k : k + 1]:
+                    finish(unit)
+            for unit in rest[runs:]:
+                finish(unit)
+        store(TOKENS // tokens_per_half - 1)

@@ -28,6 +28,7 @@ BANKS_PER_CHUNK = CHUNK // BANK
 GROUP = 4
 SIG_BANKS = 4
 FIN_BANKS = 4
+STORE_LAG = 2
 LN2 = math.log(2.0)
 LOG_FLOOR = 2.0 ** -60
 
@@ -46,9 +47,7 @@ def tile_cfconv_pa_kernel(tc, x, distances, W1, b1, W2, b2, out):
         psum_fin = ctx.enter_context(tc.psum_pool(name="psum_fin", bufs=FIN_BANKS))
 
         dist_rows = keep.tile([P, TOKENS], BF16)
-        nc.vector.memset(dist_rows[:], 0.0)
-        nc.vector.memset(dist_rows[32:33, :], 1.0)
-        nc.vector.memset(dist_rows[64:65, :], 1.0)
+        nc.vector.memset(dist_rows[:], 1.0)
         nc.sync.dma_start(out=dist_rows[0:1, :], in_=distances.rearrange("(o b) i j -> o (b i j)", o=1))
 
         w1_raw = keep.tile([P, PACK, FEATURES], BF16)
@@ -194,9 +193,12 @@ def tile_cfconv_pa_kernel(tc, x, distances, W1, b1, W2, b2, out):
                 bias=neg_bias[layer][:, ft : ft + 1],
             )
 
-        def logarithm(layer, tb, group):
+        def logarithm(layer, tb, group, pieces):
             flat = sig_tiles[(layer, tb, group)][:].rearrange("p i w -> p (i w)")
-            nc.scalar.activation(out=flat, in_=flat, func=ACT.Ln, scale=2.0, bias=log_floor[:, 0:1])
+            width = GROUP * BANK // pieces
+            for n in range(pieces):
+                part = flat[:, n * width : (n + 1) * width]
+                nc.scalar.activation(out=part, in_=part, func=ACT.Ln, scale=2.0, bias=log_floor[:, 0:1])
 
         def finish(unit):
             layer, tb, ft = unit
@@ -224,31 +226,42 @@ def tile_cfconv_pa_kernel(tc, x, distances, W1, b1, W2, b2, out):
                         in_=h_grouped[:].rearrange("p w t -> p (w t)"),
                     )
             else:
-                neg_w = work.tile([P, BANK], F32, tag="neg_w", name="neg_w", bufs=3)
+                neg_w = work.tile([P, BANK // ATOMS, ATOMS], F32, tag="neg_w", name="neg_w", bufs=4)
                 nc.vector.scalar_tensor_tensor(
-                    out=neg_w[:], in0=acc[:], scalar=shift_bias[2][:, ft : ft + 1], in1=neg_log,
+                    out=neg_w[:].rearrange("p a j -> p (a j)"), in0=acc[:], scalar=shift_bias[2][:, ft : ft + 1], in1=neg_log,
                     op0=ALU.add, op1=ALU.min,
                 )
                 pairs = BANK // ATOMS
-                nc.vector.tensor_reduce(
-                    out=neg_sums[:, ft, tb * pairs : (tb + 1) * pairs],
-                    in_=neg_w[:].rearrange("p (a j) -> p a j", j=ATOMS),
-                    axis=AXIS.X, op=ALU.add,
-                )
+                total = neg_sums[:, ft, tb * pairs : (tb + 1) * pairs]
+                if ft % 2 == 1:
+                    nc.vector.tensor_reduce(out=total, in_=neg_w[:], axis=AXIS.X, op=ALU.add)
+                else:
+                    fours = work.tile([P, pairs, 4], F32, tag="fours", name="fours")
+                    twos = work.tile([P, pairs, 2], F32, tag="twos", name="twos")
+                    nc.gpsimd.tensor_tensor(out=fours[:], in0=neg_w[:, :, 0:4], in1=neg_w[:, :, 4:8], op=ALU.add)
+                    nc.gpsimd.tensor_tensor(out=twos[:], in0=fours[:, :, 0:2], in1=fours[:, :, 2:4], op=ALU.add)
+                    nc.gpsimd.tensor_tensor(out=total, in0=twos[:, :, 0], in1=twos[:, :, 1], op=ALU.add)
 
-        def store(half):
+        def store(half, group):
             rows = slice(half * P, (half + 1) * P)
-            for group in range(FEATURE_TILES // GROUP):
-                turned = psum_fin.tile([P, GROUP, P], F32, tag="fin", name="turned")
-                for i in range(GROUP):
-                    nc.tensor.transpose(turned[:, i, :], neg_sums[:, group * GROUP + i, rows], identity[:])
-                cols = slice(group * BANK, (group + 1) * BANK)
-                result = work.tile([P, BANK], F32, tag="result", name="result")
-                nc.vector.scalar_tensor_tensor(
-                    out=result[:], in0=turned[:].rearrange("p i m -> p (i m)"), scalar=-1.0,
-                    in1=x_sb[:, half, cols], op0=ALU.mult, op1=ALU.mult,
-                )
-                nc.sync.dma_start(out=out_rows[rows, cols], in_=result[:])
+            cols = slice(group * BANK, (group + 1) * BANK)
+            turned = psum_fin.tile([P, GROUP, P], F32, tag="fin", name="turned")
+            for i in range(GROUP):
+                nc.tensor.transpose(turned[:, i, :], neg_sums[:, group * GROUP + i, rows], identity[:])
+            result = work.tile([P, BANK], F32, tag="result", name="result")
+            nc.vector.scalar_tensor_tensor(
+                out=result[:], in0=turned[:].rearrange("p i m -> p (i m)"), scalar=-1.0,
+                in1=x_sb[:, half, cols], op0=ALU.mult, op1=ALU.mult,
+            )
+            nc.sync.dma_start(out=out_rows[rows, cols], in_=result[:])
+
+        def finish_and_store(unit):
+            finish(unit)
+            layer, tb, ft = unit
+            if layer == 2 and (tb + 1) * BANK % (P * ATOMS) == 0:
+                for group in range(FEATURE_TILES // GROUP):
+                    if ft == min((group + 1) * GROUP - 1 + STORE_LAG, FEATURE_TILES - 1):
+                        store((tb + 1) * BANK // (P * ATOMS) - 1, group)
 
         def units(layer, chunk):
             if chunk < 0 or chunk >= CHUNKS:
@@ -256,30 +269,23 @@ def tile_cfconv_pa_kernel(tc, x, distances, W1, b1, W2, b2, out):
             banks = range(chunk * BANKS_PER_CHUNK, (chunk + 1) * BANKS_PER_CHUNK)
             return [(layer, tb, ft) for tb in banks for ft in range(FEATURE_TILES)]
 
-        tokens_per_half = P * ATOMS
         for unit in units(1, 0):
             sigmoid(unit)
         for r in range(CHUNKS + 1):
             first = units(1, r)
             second = units(2, r - 1)
             following = units(1, r + 1) + units(2, r)
-            for layer, tb, ft in first + second:
+            for n, (layer, tb, ft) in enumerate(first + second):
                 if ft % GROUP == 0:
-                    logarithm(layer, tb, ft // GROUP)
+                    logarithm(layer, tb, ft // GROUP, GROUP if n == 0 or r == CHUNKS else 1)
             for unit in first:
                 finish(unit)
-            done = (r - 1) * CHUNK
-            if done > 0 and done % tokens_per_half == 0:
-                store(done // tokens_per_half - 1)
-            for unit in second[:FIN_BANKS]:
-                finish(unit)
-            rest = second[FIN_BANKS:]
-            runs = len(following) // SIG_BANKS
-            for k in range(runs):
-                for later in following[k * SIG_BANKS : (k + 1) * SIG_BANKS]:
-                    sigmoid(later)
-                for unit in rest[k : k + 1]:
-                    finish(unit)
-            for unit in rest[runs:]:
-                finish(unit)
-        store(TOKENS // tokens_per_half - 1)
+            sigmoid_runs = [following[n : n + SIG_BANKS] for n in range(0, len(following), SIG_BANKS)]
+            finish_runs = [second[:FIN_BANKS]] + [[unit] for unit in second[FIN_BANKS:]]
+            for k in range(max(len(sigmoid_runs), len(finish_runs))):
+                for later in sigmoid_runs[k : k + 1]:
+                    for unit in later:
+                        sigmoid(unit)
+                for now in finish_runs[k : k + 1]:
+                    for unit in now:
+                        finish_and_store(unit)

@@ -22,13 +22,11 @@ FEATURES = 1024
 FEATURE_TILES = FEATURES // P
 BANK = 512
 BLOCK = 128
-CHUNK = 512
-CHUNKS = TOKENS // CHUNK
-BANKS_PER_CHUNK = CHUNK // BANK
+CHUNKS = TOKENS // BANK
 GROUP = 4
 SIG_BANKS = 4
 FIN_BANKS = 4
-STORE_LAG = 2
+BANKS_PER_STORE = P * ATOMS // BANK
 LN2 = math.log(2.0)
 LOG_FLOOR = 2.0 ** -60
 
@@ -255,19 +253,10 @@ def tile_cfconv_pa_kernel(tc, x, distances, W1, b1, W2, b2, out):
             )
             nc.sync.dma_start(out=out_rows[rows, cols], in_=result[:])
 
-        def finish_and_store(unit):
-            finish(unit)
-            layer, tb, ft = unit
-            if layer == 2 and (tb + 1) * BANK % (P * ATOMS) == 0:
-                for group in range(FEATURE_TILES // GROUP):
-                    if ft == min((group + 1) * GROUP - 1 + STORE_LAG, FEATURE_TILES - 1):
-                        store((tb + 1) * BANK // (P * ATOMS) - 1, group)
-
         def units(layer, chunk):
             if chunk < 0 or chunk >= CHUNKS:
                 return []
-            banks = range(chunk * BANKS_PER_CHUNK, (chunk + 1) * BANKS_PER_CHUNK)
-            return [(layer, tb, ft) for tb in banks for ft in range(FEATURE_TILES)]
+            return [(layer, chunk, ft) for ft in range(FEATURE_TILES)]
 
         for unit in units(1, 0):
             sigmoid(unit)
@@ -280,12 +269,15 @@ def tile_cfconv_pa_kernel(tc, x, distances, W1, b1, W2, b2, out):
                     logarithm(layer, tb, ft // GROUP, GROUP if n == 0 or r == CHUNKS else 1)
             for unit in first:
                 finish(unit)
-            sigmoid_runs = [following[n : n + SIG_BANKS] for n in range(0, len(following), SIG_BANKS)]
             finish_runs = [second[:FIN_BANKS]] + [[unit] for unit in second[FIN_BANKS:]]
-            for k in range(max(len(sigmoid_runs), len(finish_runs))):
+            sigmoid_runs = [following[n : n + SIG_BANKS] for n in range(0, len(following), SIG_BANKS)]
+            for k in range(max(len(finish_runs), len(sigmoid_runs))):
+                for now in finish_runs[k : k + 1]:
+                    for unit in now:
+                        finish(unit)
                 for later in sigmoid_runs[k : k + 1]:
                     for unit in later:
                         sigmoid(unit)
-                for now in finish_runs[k : k + 1]:
-                    for unit in now:
-                        finish_and_store(unit)
+            for layer, tb, ft in second:
+                if tb % BANKS_PER_STORE == BANKS_PER_STORE - 1 and ft % GROUP == GROUP - 1:
+                    store(tb // BANKS_PER_STORE, ft // GROUP)

@@ -11,24 +11,26 @@ U8 = mybir.dt.uint8
 FP8X4 = mybir.dt.float8_e4m3fn_x4
 ACT = mybir.ActivationFunctionType
 ALU = mybir.AluOpType
-AXIS = mybir.AxisListType
 
 P = 128
 PACK = 4
-TOKENS = 32 * 8 * 8
+TOKENS = 2048
 ATOMS = 8
+PAIRS = TOKENS // ATOMS
 BASIS = 512
 FEATURES = 1024
-FEATURE_TILES = FEATURES // P
+FT = FEATURES // P
 BANK = 512
 BLOCK = 128
 CHUNKS = TOKENS // BANK
 GROUP = 4
-SIG_BANKS = 4
-FIN_BANKS = 4
-BANKS_PER_STORE = P * ATOMS // BANK
 LN2 = math.log(2.0)
 LOG_FLOOR = 2.0 ** -60
+CLAMP = 2.0 ** -31
+CLAMP_LOG = 31 * LN2
+PROD_SCALE = 2.0 ** 62
+CENTRE = 256.0
+ROUND4 = 1.5 * 2.0 ** 25
 
 FLOPS = 2 * TOKENS * BASIS * FEATURES + 2 * TOKENS * FEATURES * FEATURES
 
@@ -39,128 +41,210 @@ def tile_cfconv_pa_kernel(tc, x, distances, W1, b1, W2, b2, out):
         ctx.enter_context(tc.manual_schedule())
         keep = ctx.enter_context(tc.tile_pool(name="keep", bufs=1))
         stage = ctx.enter_context(tc.tile_pool(name="stage", bufs=2))
-        sig_pool = ctx.enter_context(tc.tile_pool(name="sig_pool", bufs=6))
+        sig_pool = ctx.enter_context(tc.tile_pool(name="sig_pool", bufs=8))
         work = ctx.enter_context(tc.tile_pool(name="work", bufs=2))
-        psum_sig = ctx.enter_context(tc.psum_pool(name="psum_sig", bufs=SIG_BANKS))
-        psum_fin = ctx.enter_context(tc.psum_pool(name="psum_fin", bufs=FIN_BANKS))
+        psum_sig = ctx.enter_context(tc.psum_pool(name="psum_sig", bufs=4))
+        psum_fin = ctx.enter_context(tc.psum_pool(name="psum_fin", bufs=4))
 
-        dist_rows = keep.tile([P, TOKENS], BF16)
-        nc.vector.memset(dist_rows[:], 1.0)
-        nc.sync.dma_start(out=dist_rows[0:1, :], in_=distances.rearrange("(o b) i j -> o (b i j)", o=1))
-
+        per = TOKENS // P
+        d_bf = keep.tile([P, per], BF16)
+        nc.sync.dma_start(out=d_bf[:], in_=distances.rearrange("b i j -> (b i j)").rearrange("(p q) -> p q", q=per))
         w1_raw = keep.tile([P, PACK, FEATURES], BF16)
         nc.sync.dma_start(out=w1_raw[:], in_=W1.rearrange("(p j) f -> p j f", j=PACK))
+        b1_bf = keep.tile([P, FT], BF16)
+        b2_bf = keep.tile([P, FT], BF16)
+        x_sb = keep.tile([P, 2, FEATURES], BF16)
+        with nc.allow_non_contiguous_dma(reason="two small bias vectors"):
+            nc.sync.dma_start(
+                out=b1_bf[:].rearrange("p (g t) -> p g t", t=PACK),
+                in_=b1.rearrange("(g p t) -> p g t", p=P, t=PACK),
+            )
+            nc.sync.dma_start(out=b2_bf[:], in_=b2.rearrange("(c p) -> p c", p=P))
         w2_raw = keep.tile([P, 2, PACK, FEATURES], BF16)
         for g in range(2):
             nc.sync.dma_start(
                 out=w2_raw[:, g, :, :],
                 in_=W2[g * BASIS : (g + 1) * BASIS, :].rearrange("(p t) n -> p t n", t=PACK),
             )
-        b1_bf = keep.tile([P, FEATURE_TILES], BF16)
-        b2_bf = keep.tile([P, FEATURE_TILES], BF16)
-        x_sb = keep.tile([P, 2, FEATURES], BF16)
-        with nc.allow_non_contiguous_dma(reason="two small bias vectors, one value a partition and tile"):
-            nc.sync.dma_start(
-                out=b1_bf[:].rearrange("p (g t) -> p g t", t=PACK),
-                in_=b1.rearrange("(g p t) -> p g t", p=P, t=PACK),
-            )
-            nc.sync.dma_start(out=b2_bf[:], in_=b2.rearrange("(c p) -> p c", p=P))
-        nc.sync.dma_start(out=x_sb[:], in_=x.rearrange("(h b) i f -> (b i) h f", h=2))
+        nc.sync.dma_start(out=x_sb[:], in_=x.rearrange("b i f -> (b i) f").rearrange("(p h) f -> p h f", h=2))
 
-        centre_rows = keep.tile([P, PACK, P], BF16)
-        nc.gpsimd.memset(centre_rows[:], 0.0)
-        nc.gpsimd.memset(centre_rows[0:1, :, :], 10.0)
-        nc.gpsimd.iota(
-            centre_rows[32:33, :, :], pattern=[[0, PACK], [-PACK, P]], base=0, channel_multiplier=0,
-            allow_small_or_imprecise_dtypes=True,
-        )
-        nc.gpsimd.iota(
-            centre_rows[64:65, :, :], pattern=[[-1, PACK], [0, P]], base=0, channel_multiplier=0,
-            allow_small_or_imprecise_dtypes=True,
-        )
-        identity = keep.tile([P, P], F32)
-        make_identity(nc, identity[:])
+        cen = keep.tile([P, PACK, P], BF16)
+        nc.vector.memset(cen[:].rearrange("p j m -> p (j m)").bitcast(U32), 0)
+        rows = keep.tile([P, per, P], BF16)
+        ident_bf = keep.tile([P, P], BF16)
+        make_identity(nc, ident_bf[:])
+        kf = keep.tile([P, PACK], F32)
+        nc.gpsimd.iota(kf[:], pattern=[[1, PACK]], base=-256, channel_multiplier=PACK,
+                       allow_small_or_imprecise_dtypes=True)
+        nc.gpsimd.memset(cen[:, :, 0:2], 1.0)
+        nc.gpsimd.memset(cen[:, :, 32:35], 1.0)
+        for row in (2, 35, 36):
+            nc.gpsimd.iota(cen[:, :, row : row + 1], pattern=[[-2, PACK], [0, 1]], base=512, channel_multiplier=-2 * PACK,
+                           allow_small_or_imprecise_dtypes=True)
+        nc.vector.memset(rows[:].rearrange("p q m -> p (q m)").bitcast(U32), 0)
+        nc.vector.memset(rows[:, :, 16:18], 1.0)
+        k2 = keep.tile([P, PACK], F32)
+        nc.vector.tensor_tensor(out=k2[:], in0=kf[:], in1=kf[:], op=ALU.mult)
+        nc.vector.tensor_copy(out=cen[:, :, 16], in_=k2[:])
+        nc.vector.tensor_tensor(out=cen[:, :, 17], in0=k2[:], in1=cen[:, :, 16], op=ALU.subtract)
         log_floor = keep.tile([P, 1], F32)
         nc.vector.memset(log_floor[:], LOG_FLOOR)
+
+        cen_ps = psum_fin.tile([P, PACK, P], BF16, tag="fin", name="cen_ps")
+        for j in range(PACK):
+            nc.tensor.transpose(cen_ps[:, j, :], cen[:, j, :], ident_bf[:])
+        cen_t = keep.tile([P, PACK, P], BF16)
+        nc.scalar.copy(out=cen_t[:], in_=cen_ps[:])
+
+        dc = keep.tile([P, per], F32)
+        tt = keep.tile([P, per], F32)
+        rr = keep.tile([P, per], F32)
+        ss = keep.tile([P, per], F32)
+        cc = keep.tile([P, per], F32)
+        n2 = keep.tile([P, per], F32)
+        c2 = keep.tile([P, per], F32)
+        V = nc.vector
+        V.tensor_scalar(out=tt[:], in0=d_bf[:], scalar1=10.0, scalar2=ROUND4, op0=ALU.mult, op1=ALU.add)
+        V.tensor_scalar(out=dc[:], in0=d_bf[:], scalar1=10.0, scalar2=-CENTRE, op0=ALU.mult, op1=ALU.add)
+        V.tensor_scalar(out=rows[:, :, 2], in0=tt[:], scalar1=ROUND4 + CENTRE, scalar2=None, op0=ALU.subtract)
+        V.tensor_tensor(out=rr[:], in0=dc[:], in1=rows[:, :, 2], op=ALU.subtract)
+        V.tensor_tensor(out=ss[:], in0=dc[:], in1=rows[:, :, 2], op=ALU.add)
+        V.tensor_tensor(out=n2[:], in0=rows[:, :, 2], in1=rows[:, :, 2], op=ALU.mult)
+        V.tensor_tensor(out=cc[:], in0=rr[:], in1=ss[:], op=ALU.mult)
+        V.tensor_copy(out=rows[:, :, 35], in_=rr[:])
+        V.tensor_copy(out=rows[:, :, 0], in_=n2[:])
+        V.tensor_copy(out=rows[:, :, 32], in_=cc[:])
+        V.tensor_tensor(out=rows[:, :, 36], in0=rr[:], in1=rows[:, :, 35], op=ALU.subtract)
+        V.tensor_tensor(out=c2[:], in0=cc[:], in1=rows[:, :, 32], op=ALU.subtract)
+        V.tensor_tensor(out=rows[:, :, 1], in0=n2[:], in1=rows[:, :, 0], op=ALU.subtract)
+        V.tensor_copy(out=rows[:, :, 33], in_=c2[:])
+        V.tensor_tensor(out=rows[:, :, 34], in0=c2[:], in1=rows[:, :, 33], op=ALU.subtract)
+
+        moving = keep.tile([P, TOKENS], BF16)
+        e_bf = keep.tile([P, TOKENS, PACK], BF16, align_bytes=64)
+        e_codes = keep.tile([P, TOKENS], U32, align_bytes=64)
+        e_scales = keep.tile([P, TOKENS], U8, align_bytes=64)
+
+        def turn(c):
+            ps = psum_fin.tile([P, PACK, P], BF16, tag="fin", name="turn_ps")
+            for n in range(4):
+                jj, h = divmod(n, 2)
+                nc.tensor.transpose(ps[:, n, :], rows[:, h * ATOMS + 2 * c + jj, :], ident_bf[:])
+            dst = moving[:, c * BANK : (c + 1) * BANK].rearrange("p (n w) -> p n w", n=4)
+            if c == 0:
+                nc.scalar.copy(out=dst, in_=ps[:])
+            else:
+                nc.vector.tensor_copy(out=dst, in_=ps[:])
+
+        def basis(c):
+            for blk in range(BANK // BLOCK):
+                first = c * BANK + blk * BLOCK
+                z = psum_sig.tile([P, PACK, BLOCK], F32, tag="sig", name="z")
+                for j in range(PACK):
+                    nc.tensor.matmul(
+                        out=z[:, j, :], lhsT=cen_t[:, j, :], rhs=moving[:, first : first + BLOCK],
+                        start=True, stop=True,
+                    )
+                nc.scalar.activation(
+                    out=e_bf[:, first : first + BLOCK, :], in_=z[:].rearrange("p j w -> p w j"), func=ACT.Exp, scale=-0.1,
+                )
+
+        def quant_e(c):
+            tokens = slice(c * BANK, (c + 1) * BANK)
+            nc.vector.quantize_mx(
+                out=e_codes[:, tokens].bitcast(FP8X4), scales=e_scales[:, tokens],
+                in_=e_bf[:, tokens, :].rearrange("p w j -> p (w j)"),
+            )
 
         w1_codes = keep.tile([P, FEATURES], U32, align_bytes=64)
         w1_scales = keep.tile([P, FEATURES], U8, align_bytes=64)
         w2_codes = keep.tile([P, 2, FEATURES], U32, align_bytes=64)
         w2_scales = keep.tile([P, 2, FEATURES], U8, align_bytes=64)
-        for g in range(2):
+        grouped = {}
+
+        def w1_lay(g):
             cols = slice(g * BANK, (g + 1) * BANK)
-            grouped = stage.tile([P, PACK, P, PACK], BF16, align_bytes=64, tag="grouped", name="grouped")
+            grouped[g] = stage.tile([P, BANK, PACK], BF16, align_bytes=64, tag="grouped", name="grouped")
             nc.vector.tensor_scalar(
-                out=grouped[:], in0=w1_raw[:, :, cols].rearrange("p j (m t) -> p t m j", t=PACK),
+                out=grouped[g][:].rearrange("p (t m) j -> p t m j", t=PACK),
+                in0=w1_raw[:, :, cols].rearrange("p j (m t) -> p t m j", t=PACK),
                 scalar1=-1.0, scalar2=None, op0=ALU.mult,
             )
+
+        def w1_quant(g):
+            cols = slice(g * BANK, (g + 1) * BANK)
             nc.vector.quantize_mx(
                 out=w1_codes[:, cols].bitcast(FP8X4), scales=w1_scales[:, cols],
-                in_=grouped[:].rearrange("p t m j -> p (t m j)"),
-            )
-        for g in range(2):
-            for half in range(2):
-                cols = slice(half * BANK, (half + 1) * BANK)
-                grouped = stage.tile([P, BANK, PACK], BF16, align_bytes=64, tag="grouped", name="grouped")
-                nc.vector.tensor_scalar(
-                    out=grouped[:], in0=w2_raw[:, g, :, cols].rearrange("p t n -> p n t"),
-                    scalar1=-1.0, scalar2=None, op0=ALU.mult,
-                )
-                nc.vector.quantize_mx(
-                    out=w2_codes[:, g, cols].bitcast(FP8X4), scales=w2_scales[:, g, cols],
-                    in_=grouped[:].rearrange("p n t -> p (n t)"),
-                )
-
-        neg_bias = {}
-        shift_bias = {}
-        for layer, bias_bf in ((1, b1_bf), (2, b2_bf)):
-            neg_bias[layer] = keep.tile([P, FEATURE_TILES], F32, name="neg_bias%d" % layer)
-            shift_bias[layer] = keep.tile([P, FEATURE_TILES], F32, name="shift_bias%d" % layer)
-            nc.vector.tensor_scalar(
-                out=neg_bias[layer][:], in0=bias_bf[:], scalar1=-1.0, scalar2=None, op0=ALU.mult
-            )
-            nc.vector.tensor_scalar(
-                out=shift_bias[layer][:], in0=bias_bf[:], scalar1=-1.0, scalar2=LN2, op0=ALU.mult, op1=ALU.add
+                in_=grouped[g][:].rearrange("p n j -> p (n j)"),
             )
 
-        e_bf = keep.tile([P, TOKENS, PACK], BF16, align_bytes=64)
-        e_codes = keep.tile([P, TOKENS], U32, align_bytes=64)
-        e_scales = keep.tile([P, TOKENS], U8, align_bytes=64)
-        for tb in range(TOKENS // BANK):
-            squares = stage.tile([P, BANK // BLOCK, BLOCK, PACK], F32)
-            for blk in range(BANK // BLOCK):
-                first = tb * BANK + blk * BLOCK
-                z = psum_sig.tile([P, PACK, BLOCK], F32, tag="sig", name="z")
-                for j in range(PACK):
-                    nc.tensor.matmul(
-                        out=z[:, j, :], lhsT=centre_rows[:, j, :], rhs=dist_rows[:, first : first + BLOCK],
-                        start=True, stop=True,
-                    )
-                nc.scalar.activation(
-                    out=squares[:, blk, :, :], in_=z[:].rearrange("p j w -> p w j"), func=ACT.Square
-                )
-            tokens = slice(tb * BANK, (tb + 1) * BANK)
-            nc.scalar.activation(
-                out=e_bf[:, tokens, :].rearrange("p w j -> p (w j)"),
-                in_=squares[:].rearrange("p b w j -> p (b w j)"),
-                func=ACT.Exp,
-                scale=-0.1,
+        def w2_lay(g, half):
+            cols = slice(half * BANK, (half + 1) * BANK)
+            grouped[(g, half)] = stage.tile([P, BANK, PACK], BF16, align_bytes=64, tag="grouped", name="grouped")
+            nc.vector.tensor_scalar(
+                out=grouped[(g, half)][:], in0=w2_raw[:, g, :, cols].rearrange("p t n -> p n t"),
+                scalar1=-1.0, scalar2=None, op0=ALU.mult,
             )
+
+        def w2_quant(g, half):
+            cols = slice(half * BANK, (half + 1) * BANK)
             nc.vector.quantize_mx(
-                out=e_codes[:, tokens].bitcast(FP8X4),
-                scales=e_scales[:, tokens],
-                in_=e_bf[:, tokens, :].rearrange("p w j -> p (w j)"),
+                out=w2_codes[:, g, cols].bitcast(FP8X4), scales=w2_scales[:, g, cols],
+                in_=grouped[(g, half)][:].rearrange("p n t -> p (n t)"),
             )
+
+        turn(0)
+        turn(1)
+        basis(0)
+        turn(2)
+        turn(3)
+        for c in range(1, CHUNKS):
+            basis(c)
+        w1_lay(0)
+        w1_lay(1)
+        w1_quant(0)
+        w1_quant(1)
+        quant_e(0)
+
+        bias = {}
+
+        def bias_tile(name, src, scale, shift):
+            bias[name] = keep.tile([P, FT], F32, name=name)
+            nc.vector.tensor_scalar(
+                out=bias[name][:], in0=src[:], scalar1=scale, scalar2=shift, op0=ALU.mult, op1=ALU.add
+            )
+
+        bias_tile("neg1", b1_bf, -1.0, 0.0)
+        bias_tile("shift1", b1_bf, -1.0, LN2)
+        bias_tile("neg2", b2_bf, -1.0, 0.0)
+        bias_tile("lim2", b2_bf, 1.0, -CLAMP_LOG)
+        bias_tile("base2", b2_bf, -4.0, 66 * LN2)
+        w2_lay(0, 0)
+        quant_e(1)
+        w2_lay(0, 1)
+        w2_quant(0, 0)
+        quant_e(2)
+        w2_quant(0, 1)
+        w2_lay(1, 0)
+        quant_e(3)
+
+        w2_lay(1, 1)
+        w2_quant(1, 0)
+        w2_quant(1, 1)
+        ident = keep.tile([P, P], F32)
+        make_identity(nc, ident[:])
 
         h_codes = keep.tile([P, 2, TOKENS], U32, align_bytes=64)
         h_scales = keep.tile([P, 2, TOKENS], U8, align_bytes=64)
-        neg_sums = keep.tile([P, FEATURE_TILES, TOKENS // ATOMS], F32)
-        out_rows = out.rearrange("b i f -> (b i) f")
+        excess = keep.tile([P, FT, BANK], F32)
+        prods = keep.tile([P, 2, FT, PAIRS], F32)
         sig_tiles = {}
         neg_h_tiles = {}
+        h_tiles = {}
+        accs = {}
 
-        def product(layer, tb, ft, pool, tag):
-            tokens = slice(tb * BANK, (tb + 1) * BANK)
+        def product(layer, c, ft, pool, tag):
+            tokens = slice(c * BANK, (c + 1) * BANK)
             cols = slice(ft * P, (ft + 1) * P)
             acc = pool.tile([P, BANK], F32, tag=tag, name="acc")
             if layer == 1:
@@ -180,104 +264,151 @@ def tile_cfconv_pa_kernel(tc, x, distances, W1, b1, W2, b2, out):
                     )
             return acc
 
-        def sigmoid(unit):
-            layer, tb, ft = unit
+        def sigmoid(layer, c, ft):
             group, i = divmod(ft, GROUP)
             if i == 0:
-                sig_tiles[(layer, tb, group)] = sig_pool.tile([P, GROUP, BANK], F32, tag="sig_tile", name="sig_tile")
-            acc = product(layer, tb, ft, psum_sig, "sig")
+                sig_tiles[(layer, c, group)] = sig_pool.tile([P, GROUP, BANK], F32, tag="sig_tile", name="sig_tile")
+            if layer == 1:
+                acc = product(layer, c, ft, psum_sig, "sig")
+            else:
+                acc = product(layer, c, ft, psum_fin, "fin")
+                accs[ft] = acc
             nc.scalar.activation(
-                out=sig_tiles[(layer, tb, group)][:, i, :], in_=acc[:], func=ACT.Sigmoid,
-                bias=neg_bias[layer][:, ft : ft + 1],
+                out=sig_tiles[(layer, c, group)][:, i, :], in_=acc[:], func=ACT.Sigmoid,
+                bias=bias["neg%d" % layer][:, ft : ft + 1],
             )
 
-        def logarithm(layer, tb, group, pieces):
-            flat = sig_tiles[(layer, tb, group)][:].rearrange("p i w -> p (i w)")
+        def logarithm(c, group, pieces):
+            flat = sig_tiles[(1, c, group)][:].rearrange("p i w -> p (i w)")
             width = GROUP * BANK // pieces
             for n in range(pieces):
                 part = flat[:, n * width : (n + 1) * width]
                 nc.scalar.activation(out=part, in_=part, func=ACT.Ln, scale=2.0, bias=log_floor[:, 0:1])
 
-        def finish(unit):
-            layer, tb, ft = unit
+        def fin1(c, ft):
             group, i = divmod(ft, GROUP)
-            neg_log = sig_tiles[(layer, tb, group)][:, i, :]
-            tokens = slice(tb * BANK, (tb + 1) * BANK)
-            acc = product(layer, tb, ft, psum_fin, "fin")
-            if layer == 1:
-                if i == 0:
-                    neg_h_tiles[(tb, group)] = work.tile([P, GROUP, BANK], BF16, tag="neg_h", name="neg_h")
-                neg_h = neg_h_tiles[(tb, group)]
-                nc.vector.scalar_tensor_tensor(
-                    out=neg_h[:, i, :], in0=acc[:], scalar=shift_bias[1][:, ft : ft + 1], in1=neg_log,
-                    op0=ALU.add, op1=ALU.min,
-                )
-                if i == GROUP - 1:
-                    h_grouped = work.tile([P, BANK, PACK], BF16, align_bytes=64, tag="h_grouped", name="h_grouped")
-                    nc.vector.tensor_scalar(
-                        out=h_grouped[:], in0=neg_h[:].rearrange("p t w -> p w t"),
-                        scalar1=-1.0, scalar2=None, op0=ALU.mult,
-                    )
-                    nc.vector.quantize_mx(
-                        out=h_codes[:, group, tokens].bitcast(FP8X4),
-                        scales=h_scales[:, group, tokens],
-                        in_=h_grouped[:].rearrange("p w t -> p (w t)"),
-                    )
-            else:
-                neg_w = work.tile([P, BANK // ATOMS, ATOMS], F32, tag="neg_w", name="neg_w", bufs=4)
-                nc.vector.scalar_tensor_tensor(
-                    out=neg_w[:].rearrange("p a j -> p (a j)"), in0=acc[:], scalar=shift_bias[2][:, ft : ft + 1], in1=neg_log,
-                    op0=ALU.add, op1=ALU.min,
-                )
-                pairs = BANK // ATOMS
-                total = neg_sums[:, ft, tb * pairs : (tb + 1) * pairs]
-                if ft % 2 == 1:
-                    nc.vector.tensor_reduce(out=total, in_=neg_w[:], axis=AXIS.X, op=ALU.add)
-                else:
-                    fours = work.tile([P, pairs, 4], F32, tag="fours", name="fours")
-                    twos = work.tile([P, pairs, 2], F32, tag="twos", name="twos")
-                    nc.gpsimd.tensor_tensor(out=fours[:], in0=neg_w[:, :, 0:4], in1=neg_w[:, :, 4:8], op=ALU.add)
-                    nc.gpsimd.tensor_tensor(out=twos[:], in0=fours[:, :, 0:2], in1=fours[:, :, 2:4], op=ALU.add)
-                    nc.gpsimd.tensor_tensor(out=total, in0=twos[:, :, 0], in1=twos[:, :, 1], op=ALU.add)
+            acc = product(1, c, ft, psum_fin, "fin")
+            if i == 0:
+                neg_h_tiles[(c, group)] = work.tile([P, GROUP, BANK], BF16, tag="neg_h", name="neg_h")
+            nc.vector.scalar_tensor_tensor(
+                out=neg_h_tiles[(c, group)][:, i, :], in0=acc[:], scalar=bias["shift1"][:, ft : ft + 1],
+                in1=sig_tiles[(1, c, group)][:, i, :], op0=ALU.add, op1=ALU.min,
+            )
 
-        def store(half, group):
-            rows = slice(half * P, (half + 1) * P)
+        def lay(c, group):
+            h_tiles[(c, group)] = work.tile([P, BANK, PACK], BF16, align_bytes=64, tag="h_grouped", name="h_grouped")
+            if group == 0:
+                nc.gpsimd.tensor_scalar(
+                    out=h_tiles[(c, group)][:], in0=neg_h_tiles[(c, group)][:].rearrange("p t w -> p w t"),
+                    scalar1=-1.0, scalar2=0.0, op0=ALU.mult, op1=ALU.add,
+                )
+            else:
+                nc.vector.tensor_scalar(
+                    out=h_tiles[(c, group)][:], in0=neg_h_tiles[(c, group)][:].rearrange("p t w -> p w t"),
+                    scalar1=-1.0, scalar2=None, op0=ALU.mult,
+                )
+
+        def quant_h(c, group):
+            tokens = slice(c * BANK, (c + 1) * BANK)
+            nc.vector.quantize_mx(
+                out=h_codes[:, group, tokens].bitcast(FP8X4), scales=h_scales[:, group, tokens],
+                in_=h_tiles[(c, group)][:].rearrange("p w t -> p (w t)"),
+            )
+
+        def relu2(c, ft):
+            acc = accs[ft]
+            if c == 0:
+                nc.vector.tensor_scalar(
+                    out=excess[:, ft, :], in0=acc[:], scalar1=bias["lim2"][:, ft : ft + 1],
+                    scalar2=bias["base2"][:, ft : ft + 1], op0=ALU.min, op1=ALU.add,
+                )
+            else:
+                nc.vector.scalar_tensor_tensor(
+                    out=excess[:, ft, :], in0=acc[:], scalar=bias["lim2"][:, ft : ft + 1],
+                    in1=excess[:, ft, :], op0=ALU.min, op1=ALU.add,
+                )
+
+        def prod2(c, first, count, both=(0, 1)):
+            half = c // 2
+            group, i = divmod(first, GROUP)
+            dst = prods[:, half, first : first + count, :]
+            for jj in both:
+                src = sig_tiles[(2, c, group)][:, i : i + count, jj * PAIRS : (jj + 1) * PAIRS]
+                if c % 2 == 0 and jj == 0:
+                    nc.vector.tensor_scalar(
+                        out=dst, in0=src, scalar1=CLAMP, scalar2=PROD_SCALE, op0=ALU.max, op1=ALU.mult
+                    )
+                else:
+                    nc.vector.scalar_tensor_tensor(
+                        out=dst, in0=src, scalar=CLAMP, in1=dst, op0=ALU.max, op1=ALU.mult
+                    )
+
+        def log_prod(half, first, count):
+            part = prods[:, half, first : first + count, :].rearrange("p f a -> p (f a)")
+            nc.scalar.activation(out=part, in_=part, func=ACT.Ln)
+
+        out_rows = out.rearrange("b i f -> (b i) f").rearrange("(p h) f -> p h f", h=2)
+
+        def store(group, h):
             cols = slice(group * BANK, (group + 1) * BANK)
+            pairs = slice(h * P, (h + 1) * P)
             turned = psum_fin.tile([P, GROUP, P], F32, tag="fin", name="turned")
             for i in range(GROUP):
-                nc.tensor.transpose(turned[:, i, :], neg_sums[:, group * GROUP + i, rows], identity[:])
+                ft = group * GROUP + i
+                parts = [
+                    excess[:, ft, h * P : (h + 1) * P],
+                    excess[:, ft, PAIRS + h * P : PAIRS + (h + 1) * P],
+                    prods[:, 0, ft, pairs],
+                    prods[:, 1, ft, pairs],
+                ]
+                for n, part in enumerate(parts):
+                    nc.tensor.matmul(
+                        out=turned[:, i, :], lhsT=part, rhs=ident[:], is_transpose=True,
+                        start=(n == 0), stop=(n == len(parts) - 1),
+                    )
             result = work.tile([P, BANK], F32, tag="result", name="result")
             nc.vector.scalar_tensor_tensor(
                 out=result[:], in0=turned[:].rearrange("p i m -> p (i m)"), scalar=-1.0,
-                in1=x_sb[:, half, cols], op0=ALU.mult, op1=ALU.mult,
+                in1=x_sb[:, h, cols], op0=ALU.mult, op1=ALU.mult,
             )
-            nc.sync.dma_start(out=out_rows[rows, cols], in_=result[:])
+            nc.sync.dma_start(out=out_rows[:, h, cols], in_=result[:])
 
-        def units(layer, chunk):
-            if chunk < 0 or chunk >= CHUNKS:
-                return []
-            return [(layer, chunk, ft) for ft in range(FEATURE_TILES)]
-
-        for unit in units(1, 0):
-            sigmoid(unit)
-        for r in range(CHUNKS + 1):
-            first = units(1, r)
-            second = units(2, r - 1)
-            following = units(1, r + 1) + units(2, r)
-            for n, (layer, tb, ft) in enumerate(first + second):
-                if ft % GROUP == 0:
-                    logarithm(layer, tb, ft // GROUP, GROUP if n == 0 or r == CHUNKS else 1)
-            for unit in first:
-                finish(unit)
-            finish_runs = [second[:FIN_BANKS]] + [[unit] for unit in second[FIN_BANKS:]]
-            sigmoid_runs = [following[n : n + SIG_BANKS] for n in range(0, len(following), SIG_BANKS)]
-            for k in range(max(len(finish_runs), len(sigmoid_runs))):
-                for now in finish_runs[k : k + 1]:
-                    for unit in now:
-                        finish(unit)
-                for later in sigmoid_runs[k : k + 1]:
-                    for unit in later:
-                        sigmoid(unit)
-            for layer, tb, ft in second:
-                if tb % BANKS_PER_STORE == BANKS_PER_STORE - 1 and ft % GROUP == GROUP - 1:
-                    store(tb // BANKS_PER_STORE, ft // GROUP)
+        for ft in range(FT):
+            sigmoid(1, 0, ft)
+        for r in range(CHUNKS):
+            logarithm(r, 0, GROUP)
+            logarithm(r, 1, 2)
+            if r == CHUNKS - 1:
+                log_prod(0, 0, FT)
+            ahead = r + 1 < CHUNKS
+            if r > 0:
+                prod2(r - 1, 0, GROUP)
+            for ft in range(4):
+                fin1(r, ft)
+            if ahead:
+                for ft in range(4):
+                    sigmoid(1, r + 1, ft)
+            lay(r, 0)
+            fin1(r, 4)
+            fin1(r, 5)
+            fin1(r, 6)
+            fin1(r, 7)
+            if ahead:
+                for ft in range(4, FT):
+                    sigmoid(1, r + 1, ft)
+            quant_h(r, 0)
+            lay(r, 1)
+            quant_h(r, 1)
+            if r > 0:
+                prod2(r - 1, GROUP, GROUP, (0,))
+            for ft in range(FT):
+                sigmoid(2, r, ft)
+                relu2(r, ft)
+            if r > 0:
+                prod2(r - 1, GROUP, GROUP, (1,))
+        for first in range(0, FT, 2):
+            prod2(CHUNKS - 1, first, 2)
+            log_prod(1, first, 2)
+        for group in range(2):
+            for h in range(2):
+                store(group, h)

@@ -30,6 +30,7 @@ CLAMP = 2.0 ** -31
 CLAMP_LOG = 31 * LN2
 PROD_SCALE = 2.0 ** 62
 CENTRE = 256.0
+SPLIT = 384
 ROUND4 = 1.5 * 2.0 ** 25
 
 FLOPS = 2 * TOKENS * BASIS * FEATURES + 2 * TOKENS * FEATURES * FEATURES
@@ -271,8 +272,11 @@ def tile_cfconv_pa_kernel(tc, x, distances, W1, b1, W2, b2, out):
             if layer == 1:
                 acc = product(layer, c, ft, psum_sig, "sig")
             else:
-                acc = product(layer, c, ft, psum_fin, "fin")
-                accs[ft] = acc
+                if c == 2 and ft >= GROUP:
+                    acc = product(layer, c, ft, psum_fin, "fin")
+                else:
+                    acc = product(layer, c, ft, psum_sig, "sig")
+                accs[(c, ft)] = acc
             nc.scalar.activation(
                 out=sig_tiles[(layer, c, group)][:, i, :], in_=acc[:], func=ACT.Sigmoid,
                 bias=bias["neg%d" % layer][:, ft : ft + 1],
@@ -295,18 +299,14 @@ def tile_cfconv_pa_kernel(tc, x, distances, W1, b1, W2, b2, out):
                 in1=sig_tiles[(1, c, group)][:, i, :], op0=ALU.add, op1=ALU.min,
             )
 
-        def lay(c, group):
-            h_tiles[(c, group)] = work.tile([P, BANK, PACK], BF16, align_bytes=64, tag="h_grouped", name="h_grouped")
-            if group == 0:
-                nc.gpsimd.tensor_scalar(
-                    out=h_tiles[(c, group)][:], in0=neg_h_tiles[(c, group)][:].rearrange("p t w -> p w t"),
-                    scalar1=-1.0, scalar2=0.0, op0=ALU.mult, op1=ALU.add,
-                )
-            else:
-                nc.vector.tensor_scalar(
-                    out=h_tiles[(c, group)][:], in0=neg_h_tiles[(c, group)][:].rearrange("p t w -> p w t"),
-                    scalar1=-1.0, scalar2=None, op0=ALU.mult,
-                )
+        def lay(c, group, engine, first, last):
+            if (c, group) not in h_tiles:
+                h_tiles[(c, group)] = work.tile([P, BANK, PACK], BF16, align_bytes=64, tag="h_grouped", name="h_grouped")
+            engine.tensor_scalar(
+                out=h_tiles[(c, group)][:, first:last, :],
+                in0=neg_h_tiles[(c, group)][:, :, first:last].rearrange("p t w -> p w t"),
+                scalar1=-1.0, scalar2=0.0, op0=ALU.mult, op1=ALU.add,
+            )
 
         def quant_h(c, group):
             tokens = slice(c * BANK, (c + 1) * BANK)
@@ -316,7 +316,7 @@ def tile_cfconv_pa_kernel(tc, x, distances, W1, b1, W2, b2, out):
             )
 
         def relu2(c, ft):
-            acc = accs[ft]
+            acc = accs[(c, ft)]
             if c == 0:
                 nc.vector.tensor_scalar(
                     out=excess[:, ft, :], in0=acc[:], scalar1=bias["lim2"][:, ft : ft + 1],
@@ -328,13 +328,12 @@ def tile_cfconv_pa_kernel(tc, x, distances, W1, b1, W2, b2, out):
                     in1=excess[:, ft, :], op0=ALU.min, op1=ALU.add,
                 )
 
-        def prod2(c, first, count, both=(0, 1)):
-            half = c // 2
+        def atoms(c, first, count):
             group, i = divmod(first, GROUP)
-            dst = prods[:, half, first : first + count, :]
-            for jj in both:
-                src = sig_tiles[(2, c, group)][:, i : i + count, jj * PAIRS : (jj + 1) * PAIRS]
-                if c % 2 == 0 and jj == 0:
+            dst = prods[:, c // 2, first : first + count, :]
+            for j in range(2):
+                src = sig_tiles[(2, c, group)][:, i : i + count, j * PAIRS : (j + 1) * PAIRS]
+                if c % 2 == 0 and j == 0:
                     nc.vector.tensor_scalar(
                         out=dst, in0=src, scalar1=CLAMP, scalar2=PROD_SCALE, op0=ALU.max, op1=ALU.mult
                     )
@@ -349,66 +348,115 @@ def tile_cfconv_pa_kernel(tc, x, distances, W1, b1, W2, b2, out):
 
         out_rows = out.rearrange("b i f -> (b i) f").rearrange("(p h) f -> p h f", h=2)
 
+        turned = {}
+
+        def turn_in(group, h, parts, first, last):
+            if first:
+                turned[(group, h)] = psum_sig.tile([P, GROUP, P], F32, tag="sig", name="turned")
+            for n, (i, part) in enumerate(parts):
+                nc.tensor.matmul(
+                    out=turned[(group, h)][:, i, :], lhsT=part, rhs=ident[:], is_transpose=True,
+                    start=(first and n == 0), stop=(last and n == len(parts) - 1),
+                )
+
+        def prod_parts(part, group, h, first=0, count=GROUP):
+            return [(i, prods[:, part, group * GROUP + i, h * P : (h + 1) * P]) for i in range(first, first + count)]
+
+        def excess_parts(group, h):
+            return [
+                (i, excess[:, group * GROUP + i, j * PAIRS + h * P : j * PAIRS + (h + 1) * P])
+                for i in range(GROUP)
+                for j in range(2)
+            ]
+
         def store(group, h):
             cols = slice(group * BANK, (group + 1) * BANK)
-            pairs = slice(h * P, (h + 1) * P)
-            turned = psum_fin.tile([P, GROUP, P], F32, tag="fin", name="turned")
-            for i in range(GROUP):
-                ft = group * GROUP + i
-                parts = [
-                    excess[:, ft, h * P : (h + 1) * P],
-                    excess[:, ft, PAIRS + h * P : PAIRS + (h + 1) * P],
-                    prods[:, 0, ft, pairs],
-                    prods[:, 1, ft, pairs],
-                ]
-                for n, part in enumerate(parts):
-                    nc.tensor.matmul(
-                        out=turned[:, i, :], lhsT=part, rhs=ident[:], is_transpose=True,
-                        start=(n == 0), stop=(n == len(parts) - 1),
-                    )
-            result = work.tile([P, BANK], F32, tag="result", name="result")
+            result = work.tile([P, BANK], F32, tag="result", name="result", bufs=4)
             nc.vector.scalar_tensor_tensor(
-                out=result[:], in0=turned[:].rearrange("p i m -> p (i m)"), scalar=-1.0,
+                out=result[:], in0=turned[(group, h)][:].rearrange("p i m -> p (i m)"), scalar=-1.0,
                 in1=x_sb[:, h, cols], op0=ALU.mult, op1=ALU.mult,
             )
             nc.sync.dma_start(out=out_rows[:, h, cols], in_=result[:])
 
-        for ft in range(FT):
-            sigmoid(1, 0, ft)
-        for r in range(CHUNKS):
-            logarithm(r, 0, GROUP)
-            logarithm(r, 1, 2)
-            if r == CHUNKS - 1:
-                log_prod(0, 0, FT)
-            ahead = r + 1 < CHUNKS
-            if r > 0:
-                prod2(r - 1, 0, GROUP)
-            for ft in range(4):
-                fin1(r, ft)
-            if ahead:
-                for ft in range(4):
-                    sigmoid(1, r + 1, ft)
-            lay(r, 0)
-            fin1(r, 4)
-            fin1(r, 5)
-            fin1(r, 6)
-            fin1(r, 7)
-            if ahead:
-                for ft in range(4, FT):
-                    sigmoid(1, r + 1, ft)
-            quant_h(r, 0)
-            lay(r, 1)
-            quant_h(r, 1)
-            if r > 0:
-                prod2(r - 1, GROUP, GROUP, (0,))
+        def finish(chunks, hooks, filler=None):
+            pending = None
+            n = 0
+            for c in chunks:
+                for group in range(2):
+                    for i in range(GROUP):
+                        fin1(c, group * GROUP + i)
+                        n += 1
+                        if n in hooks:
+                            hooks[n]()
+                        if i == 2 and pending is not None:
+                            lay(*pending, nc.vector, SPLIT, BANK)
+                            quant_h(*pending)
+                    pending = (c, group)
+                    if n < len(chunks) * FT:
+                        lay(c, group, nc.gpsimd, 0, SPLIT)
+            lay(*pending, nc.vector, 0, BANK)
+            if filler is not None:
+                filler()
+            quant_h(*pending)
+
+        def logs(c):
+            logarithm(c, 0, GROUP)
+            logarithm(c, 1, 2)
+
+        def sig1(c, first, last):
+            for ft in range(first, last):
+                sigmoid(1, c, ft)
+
+        def sig2(c, first, last):
+            for ft in range(first, last):
+                sigmoid(2, c, ft)
+
+        def second(c):
+            sig2(c, 0, GROUP)
             for ft in range(FT):
-                sigmoid(2, r, ft)
-                relu2(r, ft)
-            if r > 0:
-                prod2(r - 1, GROUP, GROUP, (1,))
+                relu2(c, ft)
+                if ft + GROUP < FT:
+                    sig2(c, ft + GROUP, ft + GROUP + 1)
+
+        sig1(0, 0, FT)
+        sig1(1, 0, FT)
+        logs(0)
+        logs(1)
+        finish([0, 1], {4: lambda: sig1(2, 0, 4)})
+        sig1(2, 4, FT)
+        second(0)
+        second(1)
+        sig1(3, 0, FT)
+        for c in range(2):
+            for group in range(2):
+                atoms(c, group * GROUP, GROUP)
+        logs(2)
+        logs(3)
+        log_prod(0, 0, FT)
+        finish([2, 3], {})
+        sig2(2, 0, FT)
+        for ft in range(GROUP):
+            relu2(2, ft)
+            sig2(3, ft, ft + 1)
+        for ft in range(GROUP, FT):
+            relu2(2, ft)
+        for ft in range(GROUP):
+            relu2(3, ft)
+            sig2(3, ft + GROUP, ft + GROUP + 1)
+        for ft in range(GROUP, FT):
+            relu2(3, ft)
+        for group in range(2):
+            atoms(2, group * GROUP, GROUP)
+        for group in range(2):
+            for h in range(2):
+                turn_in(group, h, prod_parts(0, group, h), True, False)
+                turn_in(group, h, excess_parts(group, h), False, False)
         for first in range(0, FT, 2):
-            prod2(CHUNKS - 1, first, 2)
+            atoms(3, first, 2)
             log_prod(1, first, 2)
         for group in range(2):
+            for half in range(2):
+                for h in range(2):
+                    turn_in(group, h, prod_parts(1, group, h, half * 2, 2), False, half == 1)
             for h in range(2):
                 store(group, h)

@@ -30,7 +30,8 @@ CLAMP = 2.0 ** -31
 CLAMP_LOG = 31 * LN2
 PROD_SCALE = 2.0 ** 62
 CENTRE = 256.0
-SPLIT = 384
+FIRST = ((0, 2), (2, 2))
+SECOND = ((4, 2), (6, 2))
 ROUND4 = 1.5 * 2.0 ** 25
 
 FLOPS = 2 * TOKENS * BASIS * FEATURES + 2 * TOKENS * FEATURES * FEATURES
@@ -42,7 +43,7 @@ def tile_cfconv_pa_kernel(tc, x, distances, W1, b1, W2, b2, out):
         ctx.enter_context(tc.manual_schedule())
         keep = ctx.enter_context(tc.tile_pool(name="keep", bufs=1))
         stage = ctx.enter_context(tc.tile_pool(name="stage", bufs=2))
-        sig_pool = ctx.enter_context(tc.tile_pool(name="sig_pool", bufs=8))
+        sig_pool = ctx.enter_context(tc.tile_pool(name="sig_pool", bufs=12))
         work = ctx.enter_context(tc.tile_pool(name="work", bufs=2))
         psum_sig = ctx.enter_context(tc.psum_pool(name="psum_sig", bufs=4))
         psum_fin = ctx.enter_context(tc.psum_pool(name="psum_fin", bufs=4))
@@ -50,7 +51,7 @@ def tile_cfconv_pa_kernel(tc, x, distances, W1, b1, W2, b2, out):
         per = TOKENS // P
         d_bf = keep.tile([P, per], BF16)
         nc.sync.dma_start(out=d_bf[:], in_=distances.rearrange("b i j -> (b i j)").rearrange("(p q) -> p q", q=per))
-        w1_raw = keep.tile([P, PACK, FEATURES], BF16)
+        w1_raw = sig_pool.tile([P, PACK, FEATURES], BF16, tag="sig_tile", name="w1_raw")
         nc.sync.dma_start(out=w1_raw[:], in_=W1.rearrange("(p j) f -> p j f", j=PACK))
         b1_bf = keep.tile([P, FT], BF16)
         b2_bf = keep.tile([P, FT], BF16)
@@ -61,10 +62,10 @@ def tile_cfconv_pa_kernel(tc, x, distances, W1, b1, W2, b2, out):
                 in_=b1.rearrange("(g p t) -> p g t", p=P, t=PACK),
             )
             nc.sync.dma_start(out=b2_bf[:], in_=b2.rearrange("(c p) -> p c", p=P))
-        w2_raw = keep.tile([P, 2, PACK, FEATURES], BF16)
+        w2_raw = [sig_pool.tile([P, PACK, FEATURES], BF16, tag="sig_tile", name="w2_raw") for g in range(2)]
         for g in range(2):
             nc.sync.dma_start(
-                out=w2_raw[:, g, :, :],
+                out=w2_raw[g][:],
                 in_=W2[g * BASIS : (g + 1) * BASIS, :].rearrange("(p t) n -> p t n", t=PACK),
             )
         nc.sync.dma_start(out=x_sb[:], in_=x.rearrange("b i f -> (b i) f").rearrange("(p h) f -> p h f", h=2))
@@ -132,14 +133,11 @@ def tile_cfconv_pa_kernel(tc, x, distances, W1, b1, W2, b2, out):
                 jj, h = divmod(n, 2)
                 nc.tensor.transpose(ps[:, n, :], rows[:, h * ATOMS + 2 * c + jj, :], ident_bf[:])
             dst = moving[:, c * BANK : (c + 1) * BANK].rearrange("p (n w) -> p n w", n=4)
-            if c == 0:
-                nc.scalar.copy(out=dst, in_=ps[:])
-            else:
-                nc.vector.tensor_copy(out=dst, in_=ps[:])
+            nc.vector.tensor_copy(out=dst, in_=ps[:])
 
-        def basis(c):
-            for blk in range(BANK // BLOCK):
-                first = c * BANK + blk * BLOCK
+        def basis(first_block, last_block):
+            for blk in range(first_block, last_block):
+                first = blk * BLOCK
                 z = psum_sig.tile([P, PACK, BLOCK], F32, tag="sig", name="z")
                 for j in range(PACK):
                     nc.tensor.matmul(
@@ -150,8 +148,12 @@ def tile_cfconv_pa_kernel(tc, x, distances, W1, b1, W2, b2, out):
                     out=e_bf[:, first : first + BLOCK, :], in_=z[:].rearrange("p j w -> p w j"), func=ACT.Exp, scale=-0.1,
                 )
 
-        def quant_e(c):
-            tokens = slice(c * BANK, (c + 1) * BANK)
+        def span(piece):
+            plane, count = piece
+            return slice(plane * PAIRS, (plane + count) * PAIRS)
+
+        def quant_e(piece):
+            tokens = span(piece)
             nc.vector.quantize_mx(
                 out=e_codes[:, tokens].bitcast(FP8X4), scales=e_scales[:, tokens],
                 in_=e_bf[:, tokens, :].rearrange("p w j -> p (w j)"),
@@ -183,7 +185,7 @@ def tile_cfconv_pa_kernel(tc, x, distances, W1, b1, W2, b2, out):
             cols = slice(half * BANK, (half + 1) * BANK)
             grouped[(g, half)] = stage.tile([P, BANK, PACK], BF16, align_bytes=64, tag="grouped", name="grouped")
             nc.vector.tensor_scalar(
-                out=grouped[(g, half)][:], in0=w2_raw[:, g, :, cols].rearrange("p t n -> p n t"),
+                out=grouped[(g, half)][:], in0=w2_raw[g][:, :, cols].rearrange("p t n -> p n t"),
                 scalar1=-1.0, scalar2=None, op0=ALU.mult,
             )
 
@@ -196,16 +198,11 @@ def tile_cfconv_pa_kernel(tc, x, distances, W1, b1, W2, b2, out):
 
         turn(0)
         turn(1)
-        basis(0)
-        turn(2)
-        turn(3)
-        for c in range(1, CHUNKS):
-            basis(c)
+        basis(0, 8)
         w1_lay(0)
         w1_lay(1)
         w1_quant(0)
         w1_quant(1)
-        quant_e(0)
 
         bias = {}
 
@@ -220,15 +217,19 @@ def tile_cfconv_pa_kernel(tc, x, distances, W1, b1, W2, b2, out):
         bias_tile("neg2", b2_bf, -1.0, 0.0)
         bias_tile("lim2", b2_bf, 1.0, -CLAMP_LOG)
         bias_tile("base2", b2_bf, -4.0, 66 * LN2)
+        bias_tile("shift2", b2_bf, -1.0, LN2)
+        nc.vector.tensor_scalar(
+            out=bias["base2"][:, GROUP:], in0=b2_bf[:, GROUP:], scalar1=-3.0, scalar2=34 * LN2, op0=ALU.mult, op1=ALU.add
+        )
+        quant_e(FIRST[0])
+        quant_e(FIRST[1])
+        turn(2)
+        turn(3)
         w2_lay(0, 0)
-        quant_e(1)
         w2_lay(0, 1)
         w2_quant(0, 0)
-        quant_e(2)
-        w2_quant(0, 1)
         w2_lay(1, 0)
-        quant_e(3)
-
+        w2_quant(0, 1)
         w2_lay(1, 1)
         w2_quant(1, 0)
         w2_quant(1, 1)
@@ -244,10 +245,10 @@ def tile_cfconv_pa_kernel(tc, x, distances, W1, b1, W2, b2, out):
         h_tiles = {}
         accs = {}
 
-        def product(layer, c, ft, pool, tag):
-            tokens = slice(c * BANK, (c + 1) * BANK)
+        def product(layer, piece, ft, pool, tag):
+            tokens = span(piece)
             cols = slice(ft * P, (ft + 1) * P)
-            acc = pool.tile([P, BANK], F32, tag=tag, name="acc")
+            acc = pool.tile([P, piece[1] * PAIRS], F32, tag=tag, name="acc")
             if layer == 1:
                 nc.tensor.matmul_mx(
                     out=acc[:],
@@ -265,86 +266,96 @@ def tile_cfconv_pa_kernel(tc, x, distances, W1, b1, W2, b2, out):
                     )
             return acc
 
-        def sigmoid(layer, c, ft):
+        def sigmoid(layer, piece, ft, fin_bank=False):
             group, i = divmod(ft, GROUP)
             if i == 0:
-                sig_tiles[(layer, c, group)] = sig_pool.tile([P, GROUP, BANK], F32, tag="sig_tile", name="sig_tile")
-            if layer == 1:
-                acc = product(layer, c, ft, psum_sig, "sig")
+                sig_tiles[(layer, piece, group)] = sig_pool.tile(
+                    [P, GROUP, piece[1] * PAIRS], F32, tag="sig_tile", name="sig_tile"
+                )
+            if fin_bank:
+                acc = product(layer, piece, ft, psum_fin, "fin")
             else:
-                if c == 2 and ft >= GROUP:
-                    acc = product(layer, c, ft, psum_fin, "fin")
-                else:
-                    acc = product(layer, c, ft, psum_sig, "sig")
-                accs[(c, ft)] = acc
+                acc = product(layer, piece, ft, psum_sig, "sig")
+            if layer == 2:
+                accs[(piece, ft)] = acc
             nc.scalar.activation(
-                out=sig_tiles[(layer, c, group)][:, i, :], in_=acc[:], func=ACT.Sigmoid,
+                out=sig_tiles[(layer, piece, group)][:, i, :], in_=acc[:], func=ACT.Sigmoid,
                 bias=bias["neg%d" % layer][:, ft : ft + 1],
             )
 
-        def logarithm(c, group, pieces):
-            flat = sig_tiles[(1, c, group)][:].rearrange("p i w -> p (i w)")
-            width = GROUP * BANK // pieces
+        def logarithm(layer, piece, group, pieces):
+            flat = sig_tiles[(layer, piece, group)][:].rearrange("p i w -> p (i w)")
+            width = GROUP * piece[1] * PAIRS // pieces
             for n in range(pieces):
                 part = flat[:, n * width : (n + 1) * width]
                 nc.scalar.activation(out=part, in_=part, func=ACT.Ln, scale=2.0, bias=log_floor[:, 0:1])
 
-        def fin1(c, ft):
+        def fin1(piece, ft):
             group, i = divmod(ft, GROUP)
-            acc = product(1, c, ft, psum_fin, "fin")
+            acc = product(1, piece, ft, psum_fin, "fin")
             if i == 0:
-                neg_h_tiles[(c, group)] = work.tile([P, GROUP, BANK], BF16, tag="neg_h", name="neg_h")
+                neg_h_tiles[(piece, group)] = work.tile([P, GROUP, piece[1] * PAIRS], BF16, tag="neg_h", name="neg_h")
             nc.vector.scalar_tensor_tensor(
-                out=neg_h_tiles[(c, group)][:, i, :], in0=acc[:], scalar=bias["shift1"][:, ft : ft + 1],
-                in1=sig_tiles[(1, c, group)][:, i, :], op0=ALU.add, op1=ALU.min,
+                out=neg_h_tiles[(piece, group)][:, i, :], in0=acc[:], scalar=bias["shift1"][:, ft : ft + 1],
+                in1=sig_tiles[(1, piece, group)][:, i, :], op0=ALU.add, op1=ALU.min,
             )
 
-        def lay(c, group, engine, first, last):
-            if (c, group) not in h_tiles:
-                h_tiles[(c, group)] = work.tile([P, BANK, PACK], BF16, align_bytes=64, tag="h_grouped", name="h_grouped")
+        def lay(piece, group, engine, first, last):
+            if (piece, group) not in h_tiles:
+                h_tiles[(piece, group)] = work.tile(
+                    [P, piece[1] * PAIRS, PACK], BF16, align_bytes=64, tag="h_grouped", name="h_grouped"
+                )
             engine.tensor_scalar(
-                out=h_tiles[(c, group)][:, first:last, :],
-                in0=neg_h_tiles[(c, group)][:, :, first:last].rearrange("p t w -> p w t"),
+                out=h_tiles[(piece, group)][:, first:last, :],
+                in0=neg_h_tiles[(piece, group)][:, :, first:last].rearrange("p t w -> p w t"),
                 scalar1=-1.0, scalar2=0.0, op0=ALU.mult, op1=ALU.add,
             )
 
-        def quant_h(c, group):
-            tokens = slice(c * BANK, (c + 1) * BANK)
+        def quant_h(piece, group):
+            tokens = span(piece)
             nc.vector.quantize_mx(
                 out=h_codes[:, group, tokens].bitcast(FP8X4), scales=h_scales[:, group, tokens],
-                in_=h_tiles[(c, group)][:].rearrange("p w t -> p (w t)"),
+                in_=h_tiles[(piece, group)][:].rearrange("p w t -> p (w t)"),
             )
 
-        def relu2(c, ft):
-            acc = accs[(c, ft)]
-            if c == 0:
+        def relu2(piece, ft):
+            acc = accs[(piece, ft)]
+            dst = excess[:, ft, 0 : piece[1] * PAIRS]
+            if piece[0] == 0:
                 nc.vector.tensor_scalar(
-                    out=excess[:, ft, :], in0=acc[:], scalar1=bias["lim2"][:, ft : ft + 1],
+                    out=dst, in0=acc[:], scalar1=bias["lim2"][:, ft : ft + 1],
                     scalar2=bias["base2"][:, ft : ft + 1], op0=ALU.min, op1=ALU.add,
                 )
             else:
                 nc.vector.scalar_tensor_tensor(
-                    out=excess[:, ft, :], in0=acc[:], scalar=bias["lim2"][:, ft : ft + 1],
-                    in1=excess[:, ft, :], op0=ALU.min, op1=ALU.add,
+                    out=dst, in0=acc[:], scalar=bias["lim2"][:, ft : ft + 1],
+                    in1=dst, op0=ALU.min, op1=ALU.add,
                 )
 
-        def atoms(c, first, count):
+        def atoms(piece, first, count):
             group, i = divmod(first, GROUP)
-            dst = prods[:, c // 2, first : first + count, :]
-            for j in range(2):
-                src = sig_tiles[(2, c, group)][:, i : i + count, j * PAIRS : (j + 1) * PAIRS]
-                if c % 2 == 0 and j == 0:
-                    nc.vector.tensor_scalar(
-                        out=dst, in0=src, scalar1=CLAMP, scalar2=PROD_SCALE, op0=ALU.max, op1=ALU.mult
-                    )
+            for j in range(piece[1]):
+                half, place = divmod(piece[0] + j, 4)
+                dst = prods[:, half, first : first + count, :]
+                src = sig_tiles[(2, piece, group)][:, i : i + count, j * PAIRS : (j + 1) * PAIRS]
+                if place == 0:
+                    nc.vector.tensor_scalar(out=dst, in0=src, scalar1=CLAMP, scalar2=None, op0=ALU.max)
                 else:
                     nc.vector.scalar_tensor_tensor(
                         out=dst, in0=src, scalar=CLAMP, in1=dst, op0=ALU.max, op1=ALU.mult
                     )
 
+        def fin2(piece, ft):
+            group, i = divmod(ft, GROUP)
+            acc = product(2, piece, ft, psum_fin, "fin")
+            part = sig_tiles[(2, piece, group)][:, i, :]
+            nc.vector.scalar_tensor_tensor(
+                out=part, in0=acc[:], scalar=bias["shift2"][:, ft : ft + 1], in1=part, op0=ALU.add, op1=ALU.min,
+            )
+
         def log_prod(half, first, count):
             part = prods[:, half, first : first + count, :].rearrange("p f a -> p (f a)")
-            nc.scalar.activation(out=part, in_=part, func=ACT.Ln)
+            nc.scalar.activation(out=part, in_=part, func=ACT.Ln, scale=PROD_SCALE)
 
         out_rows = out.rearrange("b i f -> (b i) f").rearrange("(p h) f -> p h f", h=2)
 
@@ -369,6 +380,12 @@ def tile_cfconv_pa_kernel(tc, x, distances, W1, b1, W2, b2, out):
                 for j in range(2)
             ]
 
+        def last_parts(i, h):
+            return [
+                (i, sig_tiles[(2, SECOND[1], 1)][:, i, j * PAIRS + h * P : j * PAIRS + (h + 1) * P])
+                for j in range(2)
+            ]
+
         def store(group, h):
             cols = slice(group * BANK, (group + 1) * BANK)
             result = work.tile([P, BANK], F32, tag="result", name="result", bufs=4)
@@ -378,85 +395,85 @@ def tile_cfconv_pa_kernel(tc, x, distances, W1, b1, W2, b2, out):
             )
             nc.sync.dma_start(out=out_rows[:, h, cols], in_=result[:])
 
-        def finish(chunks, hooks, filler=None):
+        def finish(pieces, hooks):
             pending = None
             n = 0
-            for c in chunks:
+            for piece in pieces:
+                width = piece[1] * PAIRS
                 for group in range(2):
                     for i in range(GROUP):
-                        fin1(c, group * GROUP + i)
+                        fin1(piece, group * GROUP + i)
                         n += 1
                         if n in hooks:
                             hooks[n]()
                         if i == 2 and pending is not None:
-                            lay(*pending, nc.vector, SPLIT, BANK)
+                            lay(*pending, nc.vector, pending[0][1] * PAIRS * 3 // 4, pending[0][1] * PAIRS)
                             quant_h(*pending)
-                    pending = (c, group)
-                    if n < len(chunks) * FT:
-                        lay(c, group, nc.gpsimd, 0, SPLIT)
-            lay(*pending, nc.vector, 0, BANK)
-            if filler is not None:
-                filler()
+                    pending = (piece, group)
+                    if n < len(pieces) * FT:
+                        lay(piece, group, nc.gpsimd, 0, width * 3 // 4)
+            lay(*pending, nc.vector, 0, pending[0][1] * PAIRS)
             quant_h(*pending)
 
-        def logs(c):
-            logarithm(c, 0, GROUP)
-            logarithm(c, 1, 2)
+        def logs(piece):
+            logarithm(1, piece, 0, GROUP)
+            logarithm(1, piece, 1, 2)
 
-        def sig1(c, first, last):
+        def sig1(piece, first=0, last=FT):
             for ft in range(first, last):
-                sigmoid(1, c, ft)
+                sigmoid(1, piece, ft)
 
-        def sig2(c, first, last):
-            for ft in range(first, last):
-                sigmoid(2, c, ft)
+        def second(piece, bank, fts=range(FT)):
+            fts = list(fts)
+            for n in range(len(fts) + GROUP):
+                if n >= GROUP:
+                    relu2(piece, fts[n - GROUP])
+                if n < len(fts):
+                    sigmoid(2, piece, fts[n], bank)
 
-        def second(c):
-            sig2(c, 0, GROUP)
-            for ft in range(FT):
-                relu2(c, ft)
-                if ft + GROUP < FT:
-                    sig2(c, ft + GROUP, ft + GROUP + 1)
-
-        sig1(0, 0, FT)
-        sig1(1, 0, FT)
-        logs(0)
-        logs(1)
-        finish([0, 1], {4: lambda: sig1(2, 0, 4)})
-        sig1(2, 4, FT)
-        second(0)
-        second(1)
-        sig1(3, 0, FT)
-        for c in range(2):
+        for piece in FIRST:
+            sig1(piece)
+        for piece in FIRST:
+            logs(piece)
+        finish(FIRST, {10: lambda: basis(8, 12), 16: lambda: basis(12, 16)})
+        quant_e(SECOND[0])
+        quant_e(SECOND[1])
+        second(FIRST[0], False)
+        second(FIRST[1], False)
+        sig1(SECOND[0])
+        sig1(SECOND[1])
+        for piece in FIRST:
             for group in range(2):
-                atoms(c, group * GROUP, GROUP)
-        logs(2)
-        logs(3)
+                atoms(piece, group * GROUP, GROUP)
+        for piece in SECOND:
+            logs(piece)
         log_prod(0, 0, FT)
-        finish([2, 3], {})
-        sig2(2, 0, FT)
-        for ft in range(GROUP):
-            relu2(2, ft)
-            sig2(3, ft, ft + 1)
-        for ft in range(GROUP, FT):
-            relu2(2, ft)
-        for ft in range(GROUP):
-            relu2(3, ft)
-            sig2(3, ft + GROUP, ft + GROUP + 1)
-        for ft in range(GROUP, FT):
-            relu2(3, ft)
-        for group in range(2):
-            atoms(2, group * GROUP, GROUP)
+        finish(SECOND, {})
         for group in range(2):
             for h in range(2):
                 turn_in(group, h, prod_parts(0, group, h), True, False)
-                turn_in(group, h, excess_parts(group, h), False, False)
-        for first in range(0, FT, 2):
-            atoms(3, first, 2)
-            log_prod(1, first, 2)
+        second(SECOND[0], True)
+        second(SECOND[1], True, range(GROUP))
+        for ft in range(GROUP, FT):
+            sigmoid(2, SECOND[1], ft, True)
+        for group in (1, 0):
+            atoms(SECOND[0], group * GROUP, GROUP)
+        atoms(SECOND[1], 0, GROUP)
+        logarithm(2, SECOND[1], 1, GROUP)
+        log_prod(1, GROUP, GROUP)
+        log_prod(1, 0, GROUP)
+        for ft in range(GROUP, FT):
+            fin2(SECOND[1], ft)
         for group in range(2):
-            for half in range(2):
-                for h in range(2):
-                    turn_in(group, h, prod_parts(1, group, h, half * 2, 2), False, half == 1)
+            for h in range(2):
+                turn_in(group, h, excess_parts(group, h), False, False)
+        for h in range(2):
+            turn_in(0, h, prod_parts(1, 0, h), False, True)
+        for h in range(2):
+            turn_in(1, h, prod_parts(1, 1, h), False, False)
+        for i in range(GROUP):
+            for h in range(2):
+                turn_in(1, h, last_parts(i, h), False, i == GROUP - 1)
+        for group in range(2):
             for h in range(2):
                 store(group, h)

@@ -32,7 +32,7 @@ PROD_SCALE = 2.0 ** 62
 CENTRE = 256.0
 FIRST = ((0, 2), (2, 2))
 SECOND = ((4, 2), (6, 2))
-ROUND4 = 1.5 * 2.0 ** 25
+ROUND_HALF = 1.5 * 2.0 ** 22
 
 FLOPS = 2 * TOKENS * BASIS * FEATURES + 2 * TOKENS * FEATURES * FEATURES
 
@@ -61,13 +61,14 @@ def tile_cfconv_pa_kernel(tc, x, distances, W1, b1, W2, b2, out):
                 out=b1_bf[:].rearrange("p (g t) -> p g t", t=PACK),
                 in_=b1.rearrange("(g p t) -> p g t", p=P, t=PACK),
             )
-            nc.sync.dma_start(out=b2_bf[:], in_=b2.rearrange("(c p) -> p c", p=P))
         w2_raw = [sig_pool.tile([P, PACK, FEATURES], BF16, tag="sig_tile", name="w2_raw") for g in range(2)]
         for g in range(2):
             nc.sync.dma_start(
                 out=w2_raw[g][:],
                 in_=W2[g * BASIS : (g + 1) * BASIS, :].rearrange("(p t) n -> p t n", t=PACK),
             )
+        with nc.allow_non_contiguous_dma(reason="a small bias vector"):
+            nc.sync.dma_start(out=b2_bf[:], in_=b2.rearrange("(c p) -> p c", p=P))
         nc.sync.dma_start(out=x_sb[:], in_=x.rearrange("b i f -> (b i) f").rearrange("(p h) f -> p h f", h=2))
 
         cen = keep.tile([P, PACK, P], BF16)
@@ -98,28 +99,30 @@ def tile_cfconv_pa_kernel(tc, x, distances, W1, b1, W2, b2, out):
         cen_t = keep.tile([P, PACK, P], BF16)
         nc.scalar.copy(out=cen_t[:], in_=cen_ps[:])
 
-        dc = keep.tile([P, per], F32)
-        tt = keep.tile([P, per], F32)
+        near = keep.tile([P, per], F32)
+        d10 = keep.tile([P, per], F32)
+        d10s = keep.tile([P, per], F32)
         rr = keep.tile([P, per], F32)
         ss = keep.tile([P, per], F32)
         cc = keep.tile([P, per], F32)
         n2 = keep.tile([P, per], F32)
         c2 = keep.tile([P, per], F32)
         V = nc.vector
-        V.tensor_scalar(out=tt[:], in0=d_bf[:], scalar1=10.0, scalar2=ROUND4, op0=ALU.mult, op1=ALU.add)
-        V.tensor_scalar(out=dc[:], in0=d_bf[:], scalar1=10.0, scalar2=-CENTRE, op0=ALU.mult, op1=ALU.add)
-        V.tensor_scalar(out=rows[:, :, 2], in0=tt[:], scalar1=ROUND4 + CENTRE, scalar2=None, op0=ALU.subtract)
-        V.tensor_tensor(out=rr[:], in0=dc[:], in1=rows[:, :, 2], op=ALU.subtract)
-        V.tensor_tensor(out=ss[:], in0=dc[:], in1=rows[:, :, 2], op=ALU.add)
-        V.tensor_tensor(out=n2[:], in0=rows[:, :, 2], in1=rows[:, :, 2], op=ALU.mult)
+        V.tensor_scalar(out=near[:], in0=d_bf[:], scalar1=ROUND_HALF, scalar2=ROUND_HALF, op0=ALU.add, op1=ALU.subtract)
+        V.tensor_scalar(out=d10[:], in0=d_bf[:], scalar1=10.0, scalar2=None, op0=ALU.mult)
+        V.tensor_scalar(out=d10s[:], in0=d_bf[:], scalar1=10.0, scalar2=-2 * CENTRE, op0=ALU.mult, op1=ALU.add)
+        V.scalar_tensor_tensor(out=ss[:], in0=near[:], scalar=10.0, in1=d10s[:], op0=ALU.mult, op1=ALU.add)
+        V.scalar_tensor_tensor(out=rr[:], in0=near[:], scalar=-10.0, in1=d10[:], op0=ALU.mult, op1=ALU.add)
+        V.tensor_scalar(out=rows[:, :, 2], in0=near[:], scalar1=10.0, scalar2=-CENTRE, op0=ALU.mult, op1=ALU.add)
+        V.scalar_tensor_tensor(out=rows[:, :, 35], in0=near[:], scalar=-10.0, in1=d10[:], op0=ALU.mult, op1=ALU.add)
         V.tensor_tensor(out=cc[:], in0=rr[:], in1=ss[:], op=ALU.mult)
-        V.tensor_copy(out=rows[:, :, 35], in_=rr[:])
-        V.tensor_copy(out=rows[:, :, 0], in_=n2[:])
-        V.tensor_copy(out=rows[:, :, 32], in_=cc[:])
-        V.tensor_tensor(out=rows[:, :, 36], in0=rr[:], in1=rows[:, :, 35], op=ALU.subtract)
+        V.tensor_tensor(out=rows[:, :, 32], in0=rr[:], in1=ss[:], op=ALU.mult)
+        V.tensor_tensor(out=n2[:], in0=rows[:, :, 2], in1=rows[:, :, 2], op=ALU.mult)
+        V.tensor_tensor(out=rows[:, :, 0], in0=rows[:, :, 2], in1=rows[:, :, 2], op=ALU.mult)
         V.tensor_tensor(out=c2[:], in0=cc[:], in1=rows[:, :, 32], op=ALU.subtract)
+        V.tensor_tensor(out=rows[:, :, 33], in0=cc[:], in1=rows[:, :, 32], op=ALU.subtract)
+        V.tensor_tensor(out=rows[:, :, 36], in0=rr[:], in1=rows[:, :, 35], op=ALU.subtract)
         V.tensor_tensor(out=rows[:, :, 1], in0=n2[:], in1=rows[:, :, 0], op=ALU.subtract)
-        V.tensor_copy(out=rows[:, :, 33], in_=c2[:])
         V.tensor_tensor(out=rows[:, :, 34], in0=c2[:], in1=rows[:, :, 33], op=ALU.subtract)
 
         moving = keep.tile([P, TOKENS], BF16)
@@ -198,7 +201,10 @@ def tile_cfconv_pa_kernel(tc, x, distances, W1, b1, W2, b2, out):
 
         turn(0)
         turn(1)
-        basis(0, 8)
+        basis(0, 4)
+        turn(2)
+        turn(3)
+        basis(4, 16)
         w1_lay(0)
         w1_lay(1)
         w1_quant(0)
@@ -214,6 +220,18 @@ def tile_cfconv_pa_kernel(tc, x, distances, W1, b1, W2, b2, out):
 
         bias_tile("neg1", b1_bf, -1.0, 0.0)
         bias_tile("shift1", b1_bf, -1.0, LN2)
+        quant_e(FIRST[0])
+        quant_e(FIRST[1])
+        w2_lay(0, 0)
+        w2_lay(0, 1)
+        w2_quant(0, 0)
+        w2_lay(1, 0)
+        quant_e(SECOND[0])
+        w2_quant(0, 1)
+        w2_lay(1, 1)
+        w2_quant(1, 0)
+        quant_e(SECOND[1])
+        w2_quant(1, 1)
         bias_tile("neg2", b2_bf, -1.0, 0.0)
         bias_tile("lim2", b2_bf, 1.0, -CLAMP_LOG)
         bias_tile("base2", b2_bf, -4.0, 66 * LN2)
@@ -221,18 +239,6 @@ def tile_cfconv_pa_kernel(tc, x, distances, W1, b1, W2, b2, out):
         nc.vector.tensor_scalar(
             out=bias["base2"][:, GROUP:], in0=b2_bf[:, GROUP:], scalar1=-3.0, scalar2=34 * LN2, op0=ALU.mult, op1=ALU.add
         )
-        quant_e(FIRST[0])
-        quant_e(FIRST[1])
-        turn(2)
-        turn(3)
-        w2_lay(0, 0)
-        w2_lay(0, 1)
-        w2_quant(0, 0)
-        w2_lay(1, 0)
-        w2_quant(0, 1)
-        w2_lay(1, 1)
-        w2_quant(1, 0)
-        w2_quant(1, 1)
         ident = keep.tile([P, P], F32)
         make_identity(nc, ident[:])
 
@@ -332,22 +338,22 @@ def tile_cfconv_pa_kernel(tc, x, distances, W1, b1, W2, b2, out):
                     in1=dst, op0=ALU.min, op1=ALU.add,
                 )
 
-        def atoms(piece, first, count):
-            group, i = divmod(first, GROUP)
+        def atoms(piece, groups):
             for j in range(piece[1]):
                 half, place = divmod(piece[0] + j, 4)
-                dst = prods[:, half, first : first + count, :]
-                src = sig_tiles[(2, piece, group)][:, i : i + count, j * PAIRS : (j + 1) * PAIRS]
-                if place == 0:
-                    nc.vector.tensor_scalar(out=dst, in0=src, scalar1=CLAMP, scalar2=None, op0=ALU.max)
-                else:
-                    nc.vector.scalar_tensor_tensor(
-                        out=dst, in0=src, scalar=CLAMP, in1=dst, op0=ALU.max, op1=ALU.mult
-                    )
+                for group in groups:
+                    dst = prods[:, half, group * GROUP : (group + 1) * GROUP, :]
+                    src = sig_tiles[(2, piece, group)][:, :, j * PAIRS : (j + 1) * PAIRS]
+                    if place == 0:
+                        nc.vector.tensor_scalar(out=dst, in0=src, scalar1=CLAMP, scalar2=None, op0=ALU.max)
+                    else:
+                        nc.vector.scalar_tensor_tensor(
+                            out=dst, in0=src, scalar=CLAMP, in1=dst, op0=ALU.max, op1=ALU.mult
+                        )
 
         def fin2(piece, ft):
             group, i = divmod(ft, GROUP)
-            acc = product(2, piece, ft, psum_fin, "fin")
+            acc = accs[(piece, ft)]
             part = sig_tiles[(2, piece, group)][:, i, :]
             nc.vector.scalar_tensor_tensor(
                 out=part, in0=acc[:], scalar=bias["shift2"][:, ft : ft + 1], in1=part, op0=ALU.add, op1=ALU.min,
@@ -406,14 +412,13 @@ def tile_cfconv_pa_kernel(tc, x, distances, W1, b1, W2, b2, out):
                         n += 1
                         if n in hooks:
                             hooks[n]()
-                        if i == 2 and pending is not None:
+                        if i == 1 and pending is not None:
                             lay(*pending, nc.vector, pending[0][1] * PAIRS * 3 // 4, pending[0][1] * PAIRS)
+                        if i == 2 and pending is not None:
                             quant_h(*pending)
                     pending = (piece, group)
-                    if n < len(pieces) * FT:
-                        lay(piece, group, nc.gpsimd, 0, width * 3 // 4)
-            lay(*pending, nc.vector, 0, pending[0][1] * PAIRS)
-            quant_h(*pending)
+                    last = n == len(pieces) * FT
+                    lay(piece, group, nc.gpsimd, 0, width if last else width * 3 // 4)
 
         def logs(piece):
             logarithm(1, piece, 0, GROUP)
@@ -423,11 +428,13 @@ def tile_cfconv_pa_kernel(tc, x, distances, W1, b1, W2, b2, out):
             for ft in range(first, last):
                 sigmoid(1, piece, ft)
 
-        def second(piece, bank, fts=range(FT)):
+        def second(piece, bank, fts=range(FT), between=None):
             fts = list(fts)
             for n in range(len(fts) + GROUP):
                 if n >= GROUP:
                     relu2(piece, fts[n - GROUP])
+                if between is not None and n == 2 * GROUP - 1:
+                    quant_h(*between)
                 if n < len(fts):
                     sigmoid(2, piece, fts[n], bank)
 
@@ -435,16 +442,13 @@ def tile_cfconv_pa_kernel(tc, x, distances, W1, b1, W2, b2, out):
             sig1(piece)
         for piece in FIRST:
             logs(piece)
-        finish(FIRST, {10: lambda: basis(8, 12), 16: lambda: basis(12, 16)})
-        quant_e(SECOND[0])
-        quant_e(SECOND[1])
-        second(FIRST[0], False)
+        finish(FIRST, {4: lambda: sig1(SECOND[0], 0, 4)})
+        sig1(SECOND[0], 4, FT)
+        second(FIRST[0], False, between=(FIRST[1], 1))
         second(FIRST[1], False)
-        sig1(SECOND[0])
         sig1(SECOND[1])
         for piece in FIRST:
-            for group in range(2):
-                atoms(piece, group * GROUP, GROUP)
+            atoms(piece, (0, 1))
         for piece in SECOND:
             logs(piece)
         log_prod(0, 0, FT)
@@ -452,13 +456,12 @@ def tile_cfconv_pa_kernel(tc, x, distances, W1, b1, W2, b2, out):
         for group in range(2):
             for h in range(2):
                 turn_in(group, h, prod_parts(0, group, h), True, False)
-        second(SECOND[0], True)
+        second(SECOND[0], True, between=(SECOND[1], 1))
         second(SECOND[1], True, range(GROUP))
         for ft in range(GROUP, FT):
             sigmoid(2, SECOND[1], ft, True)
-        for group in (1, 0):
-            atoms(SECOND[0], group * GROUP, GROUP)
-        atoms(SECOND[1], 0, GROUP)
+        atoms(SECOND[0], (1, 0))
+        atoms(SECOND[1], (0,))
         logarithm(2, SECOND[1], 1, GROUP)
         log_prod(1, GROUP, GROUP)
         log_prod(1, 0, GROUP)
@@ -468,12 +471,13 @@ def tile_cfconv_pa_kernel(tc, x, distances, W1, b1, W2, b2, out):
             for h in range(2):
                 turn_in(group, h, excess_parts(group, h), False, False)
         for h in range(2):
-            turn_in(0, h, prod_parts(1, 0, h), False, True)
-        for h in range(2):
             turn_in(1, h, prod_parts(1, 1, h), False, False)
         for i in range(GROUP):
             for h in range(2):
                 turn_in(1, h, last_parts(i, h), False, i == GROUP - 1)
+            if i == 0:
+                for h in range(2):
+                    turn_in(0, h, prod_parts(1, 0, h), False, True)
         for group in range(2):
             for h in range(2):
                 store(group, h)

@@ -412,13 +412,13 @@ def tile_cfconv_pa_kernel(tc, x, distances, W1, b1, W2, b2, out):
                         n += 1
                         if n in hooks:
                             hooks[n]()
-                        if i == 1 and pending is not None:
-                            lay(*pending, nc.vector, pending[0][1] * PAIRS * 3 // 4, pending[0][1] * PAIRS)
                         if i == 2 and pending is not None:
+                            lay(*pending, nc.vector, pending[0][1] * PAIRS // 2, pending[0][1] * PAIRS)
+                        if i == 3 and pending is not None:
                             quant_h(*pending)
                     pending = (piece, group)
                     last = n == len(pieces) * FT
-                    lay(piece, group, nc.gpsimd, 0, width if last else width * 3 // 4)
+                    lay(piece, group, nc.gpsimd, 0, width if last else width // 2)
 
         def logs(piece):
             logarithm(1, piece, 0, GROUP)

@@ -32,6 +32,8 @@ PROD_SCALE = 2.0 ** 62
 CENTRE = 256.0
 FIRST = ((0, 2), (2, 2))
 SECOND = ((4, 2), (6, 2))
+UP = 20.0
+DOWN = 60.0
 ROUND_HALF = 1.5 * 2.0 ** 22
 
 FLOPS = 2 * TOKENS * BASIS * FEATURES + 2 * TOKENS * FEATURES * FEATURES
@@ -92,6 +94,10 @@ def tile_cfconv_pa_kernel(tc, x, distances, W1, b1, W2, b2, out):
         nc.vector.tensor_tensor(out=cen[:, :, 17], in0=k2[:], in1=cen[:, :, 16], op=ALU.subtract)
         log_floor = keep.tile([P, 1], F32)
         nc.vector.memset(log_floor[:], LOG_FLOOR)
+        up = keep.tile([P, 1], F32)
+        nc.vector.memset(up[:], UP)
+        down = keep.tile([P, 1], F32)
+        nc.vector.memset(down[:], -DOWN)
 
         cen_ps = psum_fin.tile([P, PACK, P], BF16, tag="fin", name="cen_ps")
         for j in range(PACK):
@@ -151,6 +157,33 @@ def tile_cfconv_pa_kernel(tc, x, distances, W1, b1, W2, b2, out):
                     out=e_bf[:, first : first + BLOCK, :], in_=z[:].rearrange("p j w -> p w j"), func=ACT.Exp, scale=-0.1,
                 )
 
+        cen_neg = keep.tile([P, P], BF16)
+        grown, ratio = {}, {}
+
+        def grow_start(c):
+            tokens = slice(c * BANK, (c + 1) * BANK)
+            grown[c] = sig_pool.tile([P, PACK, BANK], F32, tag="sig_tile", name="grown")
+            ratio[c] = sig_pool.tile([P, BANK], F32, tag="sig_tile", name="ratio")
+            z = psum_sig.tile([P, BANK], F32, tag="sig", name="z")
+            nc.tensor.matmul(out=z[:], lhsT=cen_t[:, 0, :], rhs=moving[:, tokens], start=True, stop=True)
+            step = psum_sig.tile([P, BANK], F32, tag="sig", name="step")
+            nc.tensor.matmul(out=step[:], lhsT=cen_t[:, 1, :], rhs=moving[:, tokens], start=True, stop=False)
+            nc.tensor.matmul(out=step[:], lhsT=cen_neg[:], rhs=moving[:, tokens], start=False, stop=True)
+            nc.scalar.activation(out=grown[c][:, 0, :], in_=z[:], func=ACT.Exp, scale=-0.1, bias=up[:, 0:1])
+            nc.scalar.activation(out=ratio[c][:], in_=step[:], func=ACT.Exp, scale=-0.1, bias=down[:, 0:1])
+
+        def grow(c, t):
+            nc.vector.scalar_tensor_tensor(
+                out=grown[c][:, t, :], in0=grown[c][:, t - 1, :], scalar=math.exp(DOWN - 0.2 * (t - 1)),
+                in1=ratio[c][:], op0=ALU.mult, op1=ALU.mult,
+            )
+
+        def e_lay(c):
+            nc.vector.tensor_scalar(
+                out=e_bf[:, c * BANK : (c + 1) * BANK, :], in0=grown[c][:].rearrange("p t w -> p w t"),
+                scalar1=math.exp(-UP), scalar2=None, op0=ALU.mult,
+            )
+
         def span(piece):
             plane, count = piece
             return slice(plane * PAIRS, (plane + count) * PAIRS)
@@ -202,11 +235,13 @@ def tile_cfconv_pa_kernel(tc, x, distances, W1, b1, W2, b2, out):
         turn(0)
         turn(1)
         basis(0, 4)
-        turn(2)
-        turn(3)
-        basis(4, 16)
         w1_lay(0)
+        turn(2)
         w1_lay(1)
+        turn(3)
+        nc.vector.tensor_scalar(out=cen_neg[:], in0=cen_t[:, 0, :], scalar1=-1.0, scalar2=None, op0=ALU.mult)
+        basis(4, 12)
+        grow_start(3)
         w1_quant(0)
         w1_quant(1)
 
@@ -226,12 +261,14 @@ def tile_cfconv_pa_kernel(tc, x, distances, W1, b1, W2, b2, out):
         w2_lay(0, 1)
         w2_quant(0, 0)
         w2_lay(1, 0)
-        quant_e(SECOND[0])
         w2_quant(0, 1)
         w2_lay(1, 1)
+        grow(3, 1)
         w2_quant(1, 0)
-        quant_e(SECOND[1])
+        grow(3, 2)
         w2_quant(1, 1)
+        quant_e(SECOND[0])
+        grow(3, 3)
         bias_tile("neg2", b2_bf, -1.0, 0.0)
         bias_tile("lim2", b2_bf, 1.0, -CLAMP_LOG)
         bias_tile("base2", b2_bf, -4.0, 66 * LN2)
@@ -239,8 +276,10 @@ def tile_cfconv_pa_kernel(tc, x, distances, W1, b1, W2, b2, out):
         nc.vector.tensor_scalar(
             out=bias["base2"][:, GROUP:], in0=b2_bf[:, GROUP:], scalar1=-3.0, scalar2=34 * LN2, op0=ALU.mult, op1=ALU.add
         )
+        e_lay(3)
         ident = keep.tile([P, P], F32)
         make_identity(nc, ident[:])
+        quant_e(SECOND[1])
 
         h_codes = keep.tile([P, 2, TOKENS], U32, align_bytes=64)
         h_scales = keep.tile([P, 2, TOKENS], U8, align_bytes=64)
@@ -272,13 +311,13 @@ def tile_cfconv_pa_kernel(tc, x, distances, W1, b1, W2, b2, out):
                     )
             return acc
 
-        def sigmoid(layer, piece, ft, fin_bank=False):
+        def sigmoid(layer, piece, ft):
             group, i = divmod(ft, GROUP)
             if i == 0:
                 sig_tiles[(layer, piece, group)] = sig_pool.tile(
                     [P, GROUP, piece[1] * PAIRS], F32, tag="sig_tile", name="sig_tile"
                 )
-            if fin_bank:
+            if layer == 2 and group == 1:
                 acc = product(layer, piece, ft, psum_fin, "fin")
             else:
                 acc = product(layer, piece, ft, psum_sig, "sig")
@@ -289,10 +328,10 @@ def tile_cfconv_pa_kernel(tc, x, distances, W1, b1, W2, b2, out):
                 bias=bias["neg%d" % layer][:, ft : ft + 1],
             )
 
-        def logarithm(layer, piece, group, pieces):
+        def logarithm(layer, piece, group, pieces, first=0, last=None):
             flat = sig_tiles[(layer, piece, group)][:].rearrange("p i w -> p (i w)")
             width = GROUP * piece[1] * PAIRS // pieces
-            for n in range(pieces):
+            for n in range(first, pieces if last is None else last):
                 part = flat[:, n * width : (n + 1) * width]
                 nc.scalar.activation(out=part, in_=part, func=ACT.Ln, scale=2.0, bias=log_floor[:, 0:1])
 
@@ -338,22 +377,18 @@ def tile_cfconv_pa_kernel(tc, x, distances, W1, b1, W2, b2, out):
                     in1=dst, op0=ALU.min, op1=ALU.add,
                 )
 
-        def atoms(piece, groups):
-            for j in range(piece[1]):
-                half, place = divmod(piece[0] + j, 4)
-                for group in groups:
-                    dst = prods[:, half, group * GROUP : (group + 1) * GROUP, :]
-                    src = sig_tiles[(2, piece, group)][:, :, j * PAIRS : (j + 1) * PAIRS]
-                    if place == 0:
-                        nc.vector.tensor_scalar(out=dst, in0=src, scalar1=CLAMP, scalar2=None, op0=ALU.max)
-                    else:
-                        nc.vector.scalar_tensor_tensor(
-                            out=dst, in0=src, scalar=CLAMP, in1=dst, op0=ALU.max, op1=ALU.mult
-                        )
+        def atom(piece, j, group):
+            half, place = divmod(piece[0] + j, 4)
+            dst = prods[:, half, group * GROUP : (group + 1) * GROUP, :]
+            src = sig_tiles[(2, piece, group)][:, :, j * PAIRS : (j + 1) * PAIRS]
+            if place == 0:
+                nc.vector.tensor_scalar(out=dst, in0=src, scalar1=CLAMP, scalar2=None, op0=ALU.max)
+            else:
+                nc.vector.scalar_tensor_tensor(out=dst, in0=src, scalar=CLAMP, in1=dst, op0=ALU.max, op1=ALU.mult)
 
         def fin2(piece, ft):
             group, i = divmod(ft, GROUP)
-            acc = accs[(piece, ft)]
+            acc = again[ft]
             part = sig_tiles[(2, piece, group)][:, i, :]
             nc.vector.scalar_tensor_tensor(
                 out=part, in0=acc[:], scalar=bias["shift2"][:, ft : ft + 1], in1=part, op0=ALU.add, op1=ALU.min,
@@ -413,12 +448,12 @@ def tile_cfconv_pa_kernel(tc, x, distances, W1, b1, W2, b2, out):
                         if n in hooks:
                             hooks[n]()
                         if i == 2 and pending is not None:
-                            lay(*pending, nc.vector, pending[0][1] * PAIRS // 2, pending[0][1] * PAIRS)
+                            lay(*pending, nc.vector, pending[0][1] * PAIRS * 9 // 16, pending[0][1] * PAIRS)
                         if i == 3 and pending is not None:
                             quant_h(*pending)
                     pending = (piece, group)
                     last = n == len(pieces) * FT
-                    lay(piece, group, nc.gpsimd, 0, width if last else width // 2)
+                    lay(piece, group, nc.gpsimd, 0, width if last else width * 9 // 16)
 
         def logs(piece):
             logarithm(1, piece, 0, GROUP)
@@ -428,15 +463,13 @@ def tile_cfconv_pa_kernel(tc, x, distances, W1, b1, W2, b2, out):
             for ft in range(first, last):
                 sigmoid(1, piece, ft)
 
-        def second(piece, bank, fts=range(FT), between=None):
-            fts = list(fts)
-            for n in range(len(fts) + GROUP):
-                if n >= GROUP:
-                    relu2(piece, fts[n - GROUP])
-                if between is not None and n == 2 * GROUP - 1:
-                    quant_h(*between)
-                if n < len(fts):
-                    sigmoid(2, piece, fts[n], bank)
+        def sig2(piece, group):
+            for i in range(GROUP):
+                sigmoid(2, piece, group * GROUP + i)
+
+        def over2(piece, group):
+            for i in range(GROUP):
+                relu2(piece, group * GROUP + i)
 
         for piece in FIRST:
             sig1(piece)
@@ -444,40 +477,72 @@ def tile_cfconv_pa_kernel(tc, x, distances, W1, b1, W2, b2, out):
             logs(piece)
         finish(FIRST, {4: lambda: sig1(SECOND[0], 0, 4)})
         sig1(SECOND[0], 4, FT)
-        second(FIRST[0], False, between=(FIRST[1], 1))
-        second(FIRST[1], False)
+        sig2(FIRST[0], 0)
+        sig2(FIRST[0], 1)
+        over2(FIRST[0], 0)
+        quant_h(FIRST[1], 1)
+        sig2(FIRST[1], 0)
+        over2(FIRST[0], 1)
+        sig2(FIRST[1], 1)
+        over2(FIRST[1], 0)
+        over2(FIRST[1], 1)
         sig1(SECOND[1])
         for piece in FIRST:
-            atoms(piece, (0, 1))
+            for j in range(piece[1]):
+                for group in range(2):
+                    atom(piece, j, group)
         for piece in SECOND:
             logs(piece)
         log_prod(0, 0, FT)
         finish(SECOND, {})
+        sig2(SECOND[0], 0)
+        sig2(SECOND[0], 1)
+        over2(SECOND[0], 0)
+        quant_h(SECOND[1], 1)
+        sig2(SECOND[1], 0)
+        over2(SECOND[0], 1)
+        sig2(SECOND[1], 1)
+        over2(SECOND[1], 0)
+        last = SECOND[1]
+        for group in range(2):
+            atom(SECOND[0], 0, group)
+        atom(SECOND[0], 1, 0)
+        atom(last, 0, 0)
+        logarithm(2, last, 1, GROUP, 0, 3)
+        again = {}
+
+        def repeat(ft):
+            again[ft] = product(2, last, ft, psum_fin, "fin")
+
+        repeat(GROUP)
         for group in range(2):
             for h in range(2):
                 turn_in(group, h, prod_parts(0, group, h), True, False)
-        second(SECOND[0], True, between=(SECOND[1], 1))
-        second(SECOND[1], True, range(GROUP))
-        for ft in range(GROUP, FT):
-            sigmoid(2, SECOND[1], ft, True)
-        atoms(SECOND[0], (1, 0))
-        atoms(SECOND[1], (0,))
-        logarithm(2, SECOND[1], 1, GROUP)
-        log_prod(1, GROUP, GROUP)
+        repeat(GROUP + 1)
+        fin2(last, GROUP)
+        atom(last, 1, 0)
         log_prod(1, 0, GROUP)
-        for ft in range(GROUP, FT):
-            fin2(SECOND[1], ft)
-        for group in range(2):
-            for h in range(2):
-                turn_in(group, h, excess_parts(group, h), False, False)
+        atom(SECOND[0], 1, 1)
+        logarithm(2, last, 1, GROUP, 3)
+        log_prod(1, GROUP, GROUP)
         for h in range(2):
-            turn_in(1, h, prod_parts(1, 1, h), False, False)
-        for i in range(GROUP):
+            turn_in(0, h, excess_parts(0, h), False, False)
+        repeat(GROUP + 2)
+        for h in range(2):
+            turn_in(1, h, excess_parts(1, h), False, False)
+        repeat(GROUP + 3)
+        for ft in range(GROUP + 1, FT):
+            fin2(last, ft)
+        for i in range(2):
             for h in range(2):
-                turn_in(1, h, last_parts(i, h), False, i == GROUP - 1)
-            if i == 0:
-                for h in range(2):
-                    turn_in(0, h, prod_parts(1, 0, h), False, True)
+                turn_in(1, h, last_parts(i, h), False, False)
+        for h in range(2):
+            turn_in(0, h, prod_parts(1, 0, h), False, True)
+        for i in range(2, GROUP):
+            for h in range(2):
+                turn_in(1, h, last_parts(i, h), False, False)
+        for h in range(2):
+            turn_in(1, h, prod_parts(1, 1, h), False, True)
         for group in range(2):
             for h in range(2):
                 store(group, h)

@@ -73,6 +73,14 @@ def tile_cfconv_pa_kernel(tc, x, distances, W1, b1, W2, b2, out):
             nc.sync.dma_start(out=b2_bf[:], in_=b2.rearrange("(c p) -> p c", p=P))
         nc.sync.dma_start(out=x_sb[:], in_=x.rearrange("b i f -> (b i) f").rearrange("(p h) f -> p h f", h=2))
 
+        blank = keep.tile([P, BANK], BF16)
+        nc.vector.memset(blank[:].bitcast(U32), 0)
+
+        def warm_up(count):
+            for n in range(count):
+                idle = psum_sig.tile([P, BANK], F32, tag="sig", name="idle")
+                nc.tensor.matmul(out=idle[:], lhsT=blank[:, 0:P], rhs=blank[:], start=True, stop=True)
+
         cen = keep.tile([P, PACK, P], BF16)
         nc.vector.memset(cen[:].rearrange("p j m -> p (j m)").bitcast(U32), 0)
         rows = keep.tile([P, per, P], BF16)
@@ -99,11 +107,13 @@ def tile_cfconv_pa_kernel(tc, x, distances, W1, b1, W2, b2, out):
         down = keep.tile([P, 1], F32)
         nc.vector.memset(down[:], -DOWN)
 
+        warm_up(5)
         cen_ps = psum_fin.tile([P, PACK, P], BF16, tag="fin", name="cen_ps")
         for j in range(PACK):
             nc.tensor.transpose(cen_ps[:, j, :], cen[:, j, :], ident_bf[:])
         cen_t = keep.tile([P, PACK, P], BF16)
         nc.scalar.copy(out=cen_t[:], in_=cen_ps[:])
+        warm_up(3)
 
         near = keep.tile([P, per], F32)
         d10 = keep.tile([P, per], F32)
@@ -142,7 +152,8 @@ def tile_cfconv_pa_kernel(tc, x, distances, W1, b1, W2, b2, out):
                 jj, h = divmod(n, 2)
                 nc.tensor.transpose(ps[:, n, :], rows[:, h * ATOMS + 2 * c + jj, :], ident_bf[:])
             dst = moving[:, c * BANK : (c + 1) * BANK].rearrange("p (n w) -> p n w", n=4)
-            nc.vector.tensor_copy(out=dst, in_=ps[:])
+            for first, last in ((0, 1), (1, 4)) if c == 0 else ((0, 4),):
+                nc.vector.tensor_copy(out=dst[:, first:last, :], in_=ps[:, first:last, :])
 
         def basis(first_block, last_block):
             for blk in range(first_block, last_block):
@@ -180,7 +191,8 @@ def tile_cfconv_pa_kernel(tc, x, distances, W1, b1, W2, b2, out):
 
         def e_lay(c):
             nc.vector.tensor_scalar(
-                out=e_bf[:, c * BANK : (c + 1) * BANK, :], in0=grown[c][:].rearrange("p t w -> p w t"),
+                out=e_bf[:, c * BANK : (c + 1) * BANK, :].rearrange("p (c i) t -> p c t i", i=4),
+                in0=grown[c][:].rearrange("p t (c i) -> p c t i", i=4),
                 scalar1=math.exp(-UP), scalar2=None, op0=ALU.mult,
             )
 
@@ -221,7 +233,8 @@ def tile_cfconv_pa_kernel(tc, x, distances, W1, b1, W2, b2, out):
             cols = slice(half * BANK, (half + 1) * BANK)
             grouped[(g, half)] = stage.tile([P, BANK, PACK], BF16, align_bytes=64, tag="grouped", name="grouped")
             nc.vector.tensor_scalar(
-                out=grouped[(g, half)][:], in0=w2_raw[g][:, :, cols].rearrange("p t n -> p n t"),
+                out=grouped[(g, half)][:].rearrange("p (c i) t -> p c t i", i=4),
+                in0=w2_raw[g][:, :, cols].rearrange("p t (c i) -> p c t i", i=4),
                 scalar1=-1.0, scalar2=None, op0=ALU.mult,
             )
 
@@ -240,7 +253,8 @@ def tile_cfconv_pa_kernel(tc, x, distances, W1, b1, W2, b2, out):
         w1_lay(1)
         turn(3)
         nc.vector.tensor_scalar(out=cen_neg[:], in0=cen_t[:, 0, :], scalar1=-1.0, scalar2=None, op0=ALU.mult)
-        basis(4, 12)
+        basis(4, 8)
+        grow_start(2)
         grow_start(3)
         w1_quant(0)
         w1_quant(1)
@@ -259,12 +273,16 @@ def tile_cfconv_pa_kernel(tc, x, distances, W1, b1, W2, b2, out):
         quant_e(FIRST[1])
         w2_lay(0, 0)
         w2_lay(0, 1)
+        grow(2, 1)
         w2_quant(0, 0)
         w2_lay(1, 0)
+        grow(2, 2)
         w2_quant(0, 1)
         w2_lay(1, 1)
+        grow(2, 3)
         grow(3, 1)
         w2_quant(1, 0)
+        e_lay(2)
         grow(3, 2)
         w2_quant(1, 1)
         quant_e(SECOND[0])
@@ -328,10 +346,10 @@ def tile_cfconv_pa_kernel(tc, x, distances, W1, b1, W2, b2, out):
                 bias=bias["neg%d" % layer][:, ft : ft + 1],
             )
 
-        def logarithm(layer, piece, group, pieces, first=0, last=None):
+        def logarithm(layer, piece, group, pieces):
             flat = sig_tiles[(layer, piece, group)][:].rearrange("p i w -> p (i w)")
             width = GROUP * piece[1] * PAIRS // pieces
-            for n in range(first, pieces if last is None else last):
+            for n in range(pieces):
                 part = flat[:, n * width : (n + 1) * width]
                 nc.scalar.activation(out=part, in_=part, func=ACT.Ln, scale=2.0, bias=log_floor[:, 0:1])
 
@@ -345,14 +363,14 @@ def tile_cfconv_pa_kernel(tc, x, distances, W1, b1, W2, b2, out):
                 in1=sig_tiles[(1, piece, group)][:, i, :], op0=ALU.add, op1=ALU.min,
             )
 
-        def lay(piece, group, engine, first, last):
+        def lay(piece, group, engine, run, first, last):
             if (piece, group) not in h_tiles:
                 h_tiles[(piece, group)] = work.tile(
                     [P, piece[1] * PAIRS, PACK], BF16, align_bytes=64, tag="h_grouped", name="h_grouped"
                 )
             engine.tensor_scalar(
-                out=h_tiles[(piece, group)][:, first:last, :],
-                in0=neg_h_tiles[(piece, group)][:, :, first:last].rearrange("p t w -> p w t"),
+                out=h_tiles[(piece, group)][:, first:last, :].rearrange("p (c i) t -> p c t i", i=run),
+                in0=neg_h_tiles[(piece, group)][:, :, first:last].rearrange("p t (c i) -> p c t i", i=run),
                 scalar1=-1.0, scalar2=0.0, op0=ALU.mult, op1=ALU.add,
             )
 
@@ -448,12 +466,12 @@ def tile_cfconv_pa_kernel(tc, x, distances, W1, b1, W2, b2, out):
                         if n in hooks:
                             hooks[n]()
                         if i == 2 and pending is not None:
-                            lay(*pending, nc.vector, pending[0][1] * PAIRS * 9 // 16, pending[0][1] * PAIRS)
+                            lay(*pending, nc.vector, 4, pending[0][1] * PAIRS * 9 // 16, pending[0][1] * PAIRS)
                         if i == 3 and pending is not None:
                             quant_h(*pending)
                     pending = (piece, group)
                     last = n == len(pieces) * FT
-                    lay(piece, group, nc.gpsimd, 0, width if last else width * 9 // 16)
+                    lay(piece, group, nc.gpsimd, 1, 0, width if last else width * 9 // 16)
 
         def logs(piece):
             logarithm(1, piece, 0, GROUP)
@@ -508,7 +526,7 @@ def tile_cfconv_pa_kernel(tc, x, distances, W1, b1, W2, b2, out):
             atom(SECOND[0], 0, group)
         atom(SECOND[0], 1, 0)
         atom(last, 0, 0)
-        logarithm(2, last, 1, GROUP, 0, 3)
+        logarithm(2, last, 1, GROUP)
         again = {}
 
         def repeat(ft):
@@ -523,7 +541,6 @@ def tile_cfconv_pa_kernel(tc, x, distances, W1, b1, W2, b2, out):
         atom(last, 1, 0)
         log_prod(1, 0, GROUP)
         atom(SECOND[0], 1, 1)
-        logarithm(2, last, 1, GROUP, 3)
         log_prod(1, GROUP, GROUP)
         for h in range(2):
             turn_in(0, h, excess_parts(0, h), False, False)

@@ -84,18 +84,19 @@ def tile_cfconv_pa_kernel(tc, x, distances, W1, b1, W2, b2, out):
         cen = keep.tile([P, PACK, P], BF16)
         nc.vector.memset(cen[:].rearrange("p j m -> p (j m)").bitcast(U32), 0)
         rows = keep.tile([P, per, P], BF16)
-        ident_bf = keep.tile([P, P], BF16)
-        make_identity(nc, ident_bf[:])
+        nc.vector.memset(rows[:].rearrange("p q m -> p (q m)").bitcast(U32), 0)
+        nc.vector.memset(rows[:, :, 16:18], 1.0)
         kf = keep.tile([P, PACK], F32)
         nc.gpsimd.iota(kf[:], pattern=[[1, PACK]], base=-256, channel_multiplier=PACK,
                        allow_small_or_imprecise_dtypes=True)
-        nc.gpsimd.memset(cen[:, :, 0:2], 1.0)
-        nc.gpsimd.memset(cen[:, :, 32:35], 1.0)
-        for row in (2, 35, 36):
-            nc.gpsimd.iota(cen[:, :, row : row + 1], pattern=[[-2, PACK], [0, 1]], base=512, channel_multiplier=-2 * PACK,
-                           allow_small_or_imprecise_dtypes=True)
-        nc.vector.memset(rows[:].rearrange("p q m -> p (q m)").bitcast(U32), 0)
-        nc.vector.memset(rows[:, :, 16:18], 1.0)
+        ident_bf = keep.tile([P, P], BF16)
+        make_identity(nc, ident_bf[:])
+        nc.vector.memset(cen[:, :, 0:2], 1.0)
+        nc.vector.memset(cen[:, :, 32:35], 1.0)
+        nc.vector.tensor_scalar(out=cen[:, :, 2], in0=kf[:], scalar1=-2.0, scalar2=None, op0=ALU.mult)
+        nc.vector.tensor_scalar(
+            out=cen[:, :, 35:37], in0=kf[:].unsqueeze(2).to_broadcast([P, PACK, 2]), scalar1=-2.0, scalar2=None, op0=ALU.mult
+        )
         k2 = keep.tile([P, PACK], F32)
         nc.vector.tensor_tensor(out=k2[:], in0=kf[:], in1=kf[:], op=ALU.mult)
         nc.vector.tensor_copy(out=cen[:, :, 16], in_=k2[:])
@@ -445,14 +446,17 @@ def tile_cfconv_pa_kernel(tc, x, distances, W1, b1, W2, b2, out):
                 for j in range(2)
             ]
 
-        def store(group, h):
-            cols = slice(group * BANK, (group + 1) * BANK)
+        def store(group, h, parts=1):
+            width = BANK // parts
             result = work.tile([P, BANK], F32, tag="result", name="result", bufs=4)
-            nc.vector.scalar_tensor_tensor(
-                out=result[:], in0=turned[(group, h)][:].rearrange("p i m -> p (i m)"), scalar=-1.0,
-                in1=x_sb[:, h, cols], op0=ALU.mult, op1=ALU.mult,
-            )
-            nc.sync.dma_start(out=out_rows[:, h, cols], in_=result[:])
+            for n in range(parts):
+                here = slice(n * width, (n + 1) * width)
+                cols = slice(group * BANK + n * width, group * BANK + (n + 1) * width)
+                nc.vector.scalar_tensor_tensor(
+                    out=result[:, here], in0=turned[(group, h)][:].rearrange("p i m -> p (i m)")[:, here], scalar=-1.0,
+                    in1=x_sb[:, h, cols], op0=ALU.mult, op1=ALU.mult,
+                )
+                nc.sync.dma_start(out=out_rows[:, h, cols], in_=result[:, here])
 
         def finish(pieces, hooks):
             pending = None
@@ -473,9 +477,10 @@ def tile_cfconv_pa_kernel(tc, x, distances, W1, b1, W2, b2, out):
                     last = n == len(pieces) * FT
                     lay(piece, group, nc.gpsimd, 1, 0, width if last else width * 9 // 16)
 
-        def logs(piece):
-            logarithm(1, piece, 0, GROUP)
-            logarithm(1, piece, 1, 2)
+        def logs(pieces):
+            for n, piece in enumerate(pieces):
+                logarithm(1, piece, 0, GROUP if n == 0 else 1)
+                logarithm(1, piece, 1, 2 if n == 0 else 1)
 
         def sig1(piece, first=0, last=FT):
             for ft in range(first, last):
@@ -491,8 +496,7 @@ def tile_cfconv_pa_kernel(tc, x, distances, W1, b1, W2, b2, out):
 
         for piece in FIRST:
             sig1(piece)
-        for piece in FIRST:
-            logs(piece)
+        logs(FIRST)
         finish(FIRST, {4: lambda: sig1(SECOND[0], 0, 4)})
         sig1(SECOND[0], 4, FT)
         sig2(FIRST[0], 0)
@@ -509,8 +513,7 @@ def tile_cfconv_pa_kernel(tc, x, distances, W1, b1, W2, b2, out):
             for j in range(piece[1]):
                 for group in range(2):
                     atom(piece, j, group)
-        for piece in SECOND:
-            logs(piece)
+        logs(SECOND)
         log_prod(0, 0, FT)
         finish(SECOND, {})
         sig2(SECOND[0], 0)
@@ -560,6 +563,7 @@ def tile_cfconv_pa_kernel(tc, x, distances, W1, b1, W2, b2, out):
                 turn_in(1, h, last_parts(i, h), False, False)
         for h in range(2):
             turn_in(1, h, prod_parts(1, 1, h), False, True)
-        for group in range(2):
-            for h in range(2):
-                store(group, h)
+        for h in range(2):
+            store(0, h)
+        store(1, 0)
+        store(1, 1, 2)

@@ -405,6 +405,15 @@ def tile_cfconv_pa_kernel(tc, x, distances, W1, b1, W2, b2, out):
             else:
                 nc.vector.scalar_tensor_tensor(out=dst, in0=src, scalar=CLAMP, in1=dst, op0=ALU.max, op1=ALU.mult)
 
+        def pair_product(piece, group):
+            src = sig_tiles[(2, piece, group)]
+            flat = src[:].rearrange("p i w -> p (i w)")
+            nc.vector.tensor_scalar(out=flat, in0=flat, scalar1=CLAMP, scalar2=None, op0=ALU.max)
+            nc.gpsimd.tensor_tensor(
+                out=prods[:, piece[0] // 4, group * GROUP : (group + 1) * GROUP, :],
+                in0=src[:, :, 0:PAIRS], in1=src[:, :, PAIRS : 2 * PAIRS], op=ALU.mult,
+            )
+
         def fin2(piece, ft):
             group, i = divmod(ft, GROUP)
             acc = again[ft]
@@ -470,12 +479,12 @@ def tile_cfconv_pa_kernel(tc, x, distances, W1, b1, W2, b2, out):
                         if n in hooks:
                             hooks[n]()
                         if i == 2 and pending is not None:
-                            lay(*pending, nc.vector, 4, pending[0][1] * PAIRS * 9 // 16, pending[0][1] * PAIRS)
+                            lay(*pending, nc.vector, 4, pending[0][1] * PAIRS // 2, pending[0][1] * PAIRS)
                         if i == 3 and pending is not None:
                             quant_h(*pending)
                     pending = (piece, group)
                     last = n == len(pieces) * FT
-                    lay(piece, group, nc.gpsimd, 1, 0, width if last else width * 9 // 16)
+                    lay(piece, group, nc.gpsimd, 1, 0, width if last else width // 2)
 
         def logs(pieces):
             for n, piece in enumerate(pieces):
@@ -521,14 +530,16 @@ def tile_cfconv_pa_kernel(tc, x, distances, W1, b1, W2, b2, out):
         over2(SECOND[0], 0)
         quant_h(SECOND[1], 1)
         sig2(SECOND[1], 0)
-        over2(SECOND[0], 1)
+        relu2(SECOND[0], 4)
+        relu2(SECOND[0], 5)
+        pair_product(SECOND[0], 0)
+        relu2(SECOND[0], 6)
+        relu2(SECOND[0], 7)
         sig2(SECOND[1], 1)
         over2(SECOND[1], 0)
         last = SECOND[1]
-        for group in range(2):
-            atom(SECOND[0], 0, group)
-        atom(SECOND[0], 1, 0)
         atom(last, 0, 0)
+        atom(SECOND[0], 0, 1)
         logarithm(2, last, 1, GROUP)
         again = {}
 

import math
from contextlib import ExitStack

import concourse.mybir as mybir
from concourse.masks import make_identity

F32 = mybir.dt.float32
BF16 = mybir.dt.bfloat16
U32 = mybir.dt.uint32
U8 = mybir.dt.uint8
FP8X4 = mybir.dt.float8_e4m3fn_x4
ACT = mybir.ActivationFunctionType
ALU = mybir.AluOpType

P = 128
PACK = 4
TOKENS = 2048
ATOMS = 8
PAIRS = TOKENS // ATOMS
BASIS = 512
FEATURES = 1024
FT = FEATURES // P
BANK = 512
BLOCK = 128
CHUNKS = TOKENS // BANK
GROUP = 4
LN2 = math.log(2.0)
LOG_FLOOR = 2.0 ** -60
CLAMP = 2.0 ** -31
CLAMP_LOG = 31 * LN2
PROD_SCALE = 2.0 ** 62
CENTRE = 256.0
FIRST = ((0, 2), (2, 2))
SECOND = ((4, 2), (6, 2))
UP = 20.0
DOWN = 60.0
ROUND_HALF = 1.5 * 2.0 ** 22

FLOPS = 2 * TOKENS * BASIS * FEATURES + 2 * TOKENS * FEATURES * FEATURES


def tile_cfconv_pa_kernel(tc, x, distances, W1, b1, W2, b2, out):
    nc = tc.nc
    with ExitStack() as ctx:
        ctx.enter_context(tc.manual_schedule())
        keep = ctx.enter_context(tc.tile_pool(name="keep", bufs=1))
        stage = ctx.enter_context(tc.tile_pool(name="stage", bufs=2))
        sig_pool = ctx.enter_context(tc.tile_pool(name="sig_pool", bufs=12))
        work = ctx.enter_context(tc.tile_pool(name="work", bufs=2))
        psum_sig = ctx.enter_context(tc.psum_pool(name="psum_sig", bufs=4))
        psum_fin = ctx.enter_context(tc.psum_pool(name="psum_fin", bufs=4))

        per = TOKENS // P
        d_bf = keep.tile([P, per], BF16)
        nc.sync.dma_start(out=d_bf[:], in_=distances.rearrange("b i j -> (b i j)").rearrange("(p q) -> p q", q=per))
        w1_raw = sig_pool.tile([P, PACK, FEATURES], BF16, tag="sig_tile", name="w1_raw")
        nc.sync.dma_start(out=w1_raw[:], in_=W1.rearrange("(p j) f -> p j f", j=PACK))
        b1_bf = keep.tile([P, FT], BF16)
        b2_bf = keep.tile([P, FT], BF16)
        x_sb = keep.tile([P, 2, FEATURES], BF16)
        with nc.allow_non_contiguous_dma(reason="two small bias vectors"):
            nc.sync.dma_start(
                out=b1_bf[:].rearrange("p (g t) -> p g t", t=PACK),
                in_=b1.rearrange("(g p t) -> p g t", p=P, t=PACK),
            )
        w2_raw = [sig_pool.tile([P, PACK, FEATURES], BF16, tag="sig_tile", name="w2_raw") for g in range(2)]
        for g in range(2):
            nc.sync.dma_start(
                out=w2_raw[g][:],
                in_=W2[g * BASIS : (g + 1) * BASIS, :].rearrange("(p t) n -> p t n", t=PACK),
            )
        with nc.allow_non_contiguous_dma(reason="a small bias vector"):
            nc.sync.dma_start(out=b2_bf[:], in_=b2.rearrange("(c p) -> p c", p=P))
        nc.sync.dma_start(out=x_sb[:], in_=x.rearrange("b i f -> (b i) f").rearrange("(p h) f -> p h f", h=2))

        blank = keep.tile([P, BANK], BF16)
        nc.vector.memset(blank[:].bitcast(U32), 0)

        def warm_up(count):
            for n in range(count):
                idle = psum_sig.tile([P, BANK], F32, tag="sig", name="idle")
                nc.tensor.matmul(out=idle[:], lhsT=blank[:, 0:P], rhs=blank[:], start=True, stop=True)

        cen = keep.tile([P, PACK, P], BF16)
        nc.vector.memset(cen[:].rearrange("p j m -> p (j m)").bitcast(U32), 0)
        rows = keep.tile([P, per, P], BF16)
        nc.vector.memset(rows[:].rearrange("p q m -> p (q m)").bitcast(U32), 0)
        nc.vector.memset(rows[:, :, 16:18], 1.0)
        kf = keep.tile([P, PACK], F32)
        nc.gpsimd.iota(kf[:], pattern=[[1, PACK]], base=-256, channel_multiplier=PACK,
                       allow_small_or_imprecise_dtypes=True)
        ident_bf = keep.tile([P, P], BF16)
        make_identity(nc, ident_bf[:])
        nc.vector.memset(cen[:, :, 0:2], 1.0)
        nc.vector.memset(cen[:, :, 32:35], 1.0)
        nc.vector.tensor_scalar(out=cen[:, :, 2], in0=kf[:], scalar1=-2.0, scalar2=None, op0=ALU.mult)
        nc.vector.tensor_scalar(
            out=cen[:, :, 35:37], in0=kf[:].unsqueeze(2).to_broadcast([P, PACK, 2]), scalar1=-2.0, scalar2=None, op0=ALU.mult
        )
        k2 = keep.tile([P, PACK], F32)
        nc.vector.tensor_tensor(out=k2[:], in0=kf[:], in1=kf[:], op=ALU.mult)
        nc.vector.tensor_copy(out=cen[:, :, 16], in_=k2[:])
        nc.vector.tensor_tensor(out=cen[:, :, 17], in0=k2[:], in1=cen[:, :, 16], op=ALU.subtract)
        log_floor = keep.tile([P, 1], F32)
        nc.vector.memset(log_floor[:], LOG_FLOOR)
        up = keep.tile([P, 1], F32)
        nc.vector.memset(up[:], UP)
        down = keep.tile([P, 1], F32)
        nc.vector.memset(down[:], -DOWN)

        warm_up(5)
        cen_ps = psum_fin.tile([P, PACK, P], BF16, tag="fin", name="cen_ps")
        for j in range(PACK):
            nc.tensor.transpose(cen_ps[:, j, :], cen[:, j, :], ident_bf[:])
        cen_t = keep.tile([P, PACK, P], BF16)
        nc.scalar.copy(out=cen_t[:], in_=cen_ps[:])
        warm_up(3)

        near = keep.tile([P, per], F32)
        d10 = keep.tile([P, per], F32)
        d10s = keep.tile([P, per], F32)
        rr = keep.tile([P, per], F32)
        ss = keep.tile([P, per], F32)
        cc = keep.tile([P, per], F32)
        n2 = keep.tile([P, per], F32)
        c2 = keep.tile([P, per], F32)
        V = nc.vector
        V.tensor_scalar(out=near[:], in0=d_bf[:], scalar1=ROUND_HALF, scalar2=ROUND_HALF, op0=ALU.add, op1=ALU.subtract)
        V.tensor_scalar(out=d10[:], in0=d_bf[:], scalar1=10.0, scalar2=None, op0=ALU.mult)
        V.tensor_scalar(out=d10s[:], in0=d_bf[:], scalar1=10.0, scalar2=-2 * CENTRE, op0=ALU.mult, op1=ALU.add)
        V.scalar_tensor_tensor(out=ss[:], in0=near[:], scalar=10.0, in1=d10s[:], op0=ALU.mult, op1=ALU.add)
        V.scalar_tensor_tensor(out=rr[:], in0=near[:], scalar=-10.0, in1=d10[:], op0=ALU.mult, op1=ALU.add)
        V.tensor_scalar(out=rows[:, :, 2], in0=near[:], scalar1=10.0, scalar2=-CENTRE, op0=ALU.mult, op1=ALU.add)
        V.scalar_tensor_tensor(out=rows[:, :, 35], in0=near[:], scalar=-10.0, in1=d10[:], op0=ALU.mult, op1=ALU.add)
        V.tensor_tensor(out=cc[:], in0=rr[:], in1=ss[:], op=ALU.mult)
        V.tensor_tensor(out=rows[:, :, 32], in0=rr[:], in1=ss[:], op=ALU.mult)
        V.tensor_tensor(out=n2[:], in0=rows[:, :, 2], in1=rows[:, :, 2], op=ALU.mult)
        V.tensor_tensor(out=rows[:, :, 0], in0=rows[:, :, 2], in1=rows[:, :, 2], op=ALU.mult)
        V.tensor_tensor(out=c2[:], in0=cc[:], in1=rows[:, :, 32], op=ALU.subtract)
        V.tensor_tensor(out=rows[:, :, 33], in0=cc[:], in1=rows[:, :, 32], op=ALU.subtract)
        V.tensor_tensor(out=rows[:, :, 36], in0=rr[:], in1=rows[:, :, 35], op=ALU.subtract)
        V.tensor_tensor(out=rows[:, :, 1], in0=n2[:], in1=rows[:, :, 0], op=ALU.subtract)
        V.tensor_tensor(out=rows[:, :, 34], in0=c2[:], in1=rows[:, :, 33], op=ALU.subtract)

        moving = keep.tile([P, TOKENS], BF16)
        e_bf = keep.tile([P, TOKENS, PACK], BF16, align_bytes=64)
        e_codes = keep.tile([P, TOKENS], U32, align_bytes=64)
        e_scales = keep.tile([P, TOKENS], U8, align_bytes=64)

        def turn(c):
            ps = psum_fin.tile([P, PACK, P], BF16, tag="fin", name="turn_ps")
            for n in range(4):
                jj, h = divmod(n, 2)
                nc.tensor.transpose(ps[:, n, :], rows[:, h * ATOMS + 2 * c + jj, :], ident_bf[:])
            dst = moving[:, c * BANK : (c + 1) * BANK].rearrange("p (n w) -> p n w", n=4)
            for first, last in ((0, 1), (1, 4)) if c == 0 else ((0, 4),):
                nc.vector.tensor_copy(out=dst[:, first:last, :], in_=ps[:, first:last, :])

        def basis(first_block, last_block):
            for blk in range(first_block, last_block):
                first = blk * BLOCK
                z = psum_sig.tile([P, PACK, BLOCK], F32, tag="sig", name="z")
                for j in range(PACK):
                    nc.tensor.matmul(
                        out=z[:, j, :], lhsT=cen_t[:, j, :], rhs=moving[:, first : first + BLOCK],
                        start=True, stop=True,
                    )
                nc.scalar.activation(
                    out=e_bf[:, first : first + BLOCK, :], in_=z[:].rearrange("p j w -> p w j"), func=ACT.Exp, scale=-0.1,
                )

        cen_neg = keep.tile([P, P], BF16)
        grown, ratio = {}, {}

        def grow_start(c):
            tokens = slice(c * BANK, (c + 1) * BANK)
            grown[c] = sig_pool.tile([P, PACK, BANK], F32, tag="sig_tile", name="grown")
            ratio[c] = sig_pool.tile([P, BANK], F32, tag="sig_tile", name="ratio")
            z = psum_sig.tile([P, BANK], F32, tag="sig", name="z")
            nc.tensor.matmul(out=z[:], lhsT=cen_t[:, 0, :], rhs=moving[:, tokens], start=True, stop=True)
            step = psum_sig.tile([P, BANK], F32, tag="sig", name="step")
            nc.tensor.matmul(out=step[:], lhsT=cen_t[:, 1, :], rhs=moving[:, tokens], start=True, stop=False)
            nc.tensor.matmul(out=step[:], lhsT=cen_neg[:], rhs=moving[:, tokens], start=False, stop=True)
            nc.scalar.activation(out=grown[c][:, 0, :], in_=z[:], func=ACT.Exp, scale=-0.1, bias=up[:, 0:1])
            nc.scalar.activation(out=ratio[c][:], in_=step[:], func=ACT.Exp, scale=-0.1, bias=down[:, 0:1])

        def grow(c, t):
            nc.vector.scalar_tensor_tensor(
                out=grown[c][:, t, :], in0=grown[c][:, t - 1, :], scalar=math.exp(DOWN - 0.2 * (t - 1)),
                in1=ratio[c][:], op0=ALU.mult, op1=ALU.mult,
            )

        def e_lay(c):
            nc.vector.tensor_scalar(
                out=e_bf[:, c * BANK : (c + 1) * BANK, :].rearrange("p (c i) t -> p c t i", i=4),
                in0=grown[c][:].rearrange("p t (c i) -> p c t i", i=4),
                scalar1=math.exp(-UP), scalar2=None, op0=ALU.mult,
            )

        def span(piece):
            plane, count = piece
            return slice(plane * PAIRS, (plane + count) * PAIRS)

        def quant_e(piece):
            tokens = span(piece)
            nc.vector.quantize_mx(
                out=e_codes[:, tokens].bitcast(FP8X4), scales=e_scales[:, tokens],
                in_=e_bf[:, tokens, :].rearrange("p w j -> p (w j)"),
            )

        w1_codes = keep.tile([P, FEATURES], U32, align_bytes=64)
        w1_scales = keep.tile([P, FEATURES], U8, align_bytes=64)
        w2_codes = keep.tile([P, 2, FEATURES], U32, align_bytes=64)
        w2_scales = keep.tile([P, 2, FEATURES], U8, align_bytes=64)
        grouped = {}

        def w1_lay(g):
            cols = slice(g * BANK, (g + 1) * BANK)
            grouped[g] = stage.tile([P, BANK, PACK], BF16, align_bytes=64, tag="grouped", name="grouped")
            nc.vector.tensor_scalar(
                out=grouped[g][:].rearrange("p (t m) j -> p t m j", t=PACK),
                in0=w1_raw[:, :, cols].rearrange("p j (m t) -> p t m j", t=PACK),
                scalar1=-1.0, scalar2=None, op0=ALU.mult,
            )

        def w1_quant(g):
            cols = slice(g * BANK, (g + 1) * BANK)
            nc.vector.quantize_mx(
                out=w1_codes[:, cols].bitcast(FP8X4), scales=w1_scales[:, cols],
                in_=grouped[g][:].rearrange("p n j -> p (n j)"),
            )

        def w2_lay(g, half):
            cols = slice(half * BANK, (half + 1) * BANK)
            grouped[(g, half)] = stage.tile([P, BANK, PACK], BF16, align_bytes=64, tag="grouped", name="grouped")
            nc.vector.tensor_scalar(
                out=grouped[(g, half)][:].rearrange("p (c i) t -> p c t i", i=4),
                in0=w2_raw[g][:, :, cols].rearrange("p t (c i) -> p c t i", i=4),
                scalar1=-1.0, scalar2=None, op0=ALU.mult,
            )

        def w2_quant(g, half):
            cols = slice(half * BANK, (half + 1) * BANK)
            nc.vector.quantize_mx(
                out=w2_codes[:, g, cols].bitcast(FP8X4), scales=w2_scales[:, g, cols],
                in_=grouped[(g, half)][:].rearrange("p n t -> p (n t)"),
            )

        turn(0)
        turn(1)
        basis(0, 4)
        w1_lay(0)
        turn(2)
        w1_lay(1)
        turn(3)
        nc.vector.tensor_scalar(out=cen_neg[:], in0=cen_t[:, 0, :], scalar1=-1.0, scalar2=None, op0=ALU.mult)
        basis(4, 8)
        grow_start(2)
        grow_start(3)
        w1_quant(0)
        w1_quant(1)

        bias = {}

        def bias_tile(name, src, scale, shift):
            bias[name] = keep.tile([P, FT], F32, name=name)
            nc.vector.tensor_scalar(
                out=bias[name][:], in0=src[:], scalar1=scale, scalar2=shift, op0=ALU.mult, op1=ALU.add
            )

        bias_tile("neg1", b1_bf, -1.0, 0.0)
        bias_tile("shift1", b1_bf, -1.0, LN2)
        quant_e(FIRST[0])
        quant_e(FIRST[1])
        w2_lay(0, 0)
        w2_lay(0, 1)
        grow(2, 1)
        w2_quant(0, 0)
        w2_lay(1, 0)
        grow(2, 2)
        w2_quant(0, 1)
        w2_lay(1, 1)
        grow(2, 3)
        grow(3, 1)
        w2_quant(1, 0)
        e_lay(2)
        grow(3, 2)
        w2_quant(1, 1)
        quant_e(SECOND[0])
        grow(3, 3)
        bias_tile("neg2", b2_bf, -1.0, 0.0)
        bias_tile("lim2", b2_bf, 1.0, -CLAMP_LOG)
        bias_tile("base2", b2_bf, -4.0, 66 * LN2)
        bias_tile("shift2", b2_bf, -1.0, LN2)
        nc.vector.tensor_scalar(
            out=bias["base2"][:, GROUP:], in0=b2_bf[:, GROUP:], scalar1=-3.0, scalar2=34 * LN2, op0=ALU.mult, op1=ALU.add
        )
        e_lay(3)
        ident = keep.tile([P, P], F32)
        make_identity(nc, ident[:])
        quant_e(SECOND[1])

        h_codes = keep.tile([P, 2, TOKENS], U32, align_bytes=64)
        h_scales = keep.tile([P, 2, TOKENS], U8, align_bytes=64)
        excess = keep.tile([P, FT, BANK], F32)
        prods = keep.tile([P, 2, FT, PAIRS], F32)
        sig_tiles = {}
        neg_h_tiles = {}
        h_tiles = {}
        accs = {}

        def product(layer, piece, ft, pool, tag):
            tokens = span(piece)
            cols = slice(ft * P, (ft + 1) * P)
            acc = pool.tile([P, piece[1] * PAIRS], F32, tag=tag, name="acc")
            if layer == 1:
                nc.tensor.matmul_mx(
                    out=acc[:],
                    lhsT=w1_codes[:, cols].bitcast(FP8X4), lhsT_scale=w1_scales[:, cols],
                    rhs=e_codes[:, tokens].bitcast(FP8X4), rhs_scale=e_scales[:, tokens],
                    start=True, stop=True,
                )
            else:
                for g in range(2):
                    nc.tensor.matmul_mx(
                        out=acc[:],
                        lhsT=w2_codes[:, g, cols].bitcast(FP8X4), lhsT_scale=w2_scales[:, g, cols],
                        rhs=h_codes[:, g, tokens].bitcast(FP8X4), rhs_scale=h_scales[:, g, tokens],
                        start=(g == 0), stop=(g == 1),
                    )
            return acc

        def sigmoid(layer, piece, ft):
            group, i = divmod(ft, GROUP)
            if i == 0:
                sig_tiles[(layer, piece, group)] = sig_pool.tile(
                    [P, GROUP, piece[1] * PAIRS], F32, tag="sig_tile", name="sig_tile"
                )
            if layer == 2 and group == 1:
                acc = product(layer, piece, ft, psum_fin, "fin")
            else:
                acc = product(layer, piece, ft, psum_sig, "sig")
            if layer == 2:
                accs[(piece, ft)] = acc
            nc.scalar.activation(
                out=sig_tiles[(layer, piece, group)][:, i, :], in_=acc[:], func=ACT.Sigmoid,
                bias=bias["neg%d" % layer][:, ft : ft + 1],
            )

        def logarithm(layer, piece, group, pieces):
            flat = sig_tiles[(layer, piece, group)][:].rearrange("p i w -> p (i w)")
            width = GROUP * piece[1] * PAIRS // pieces
            for n in range(pieces):
                part = flat[:, n * width : (n + 1) * width]
                nc.scalar.activation(out=part, in_=part, func=ACT.Ln, scale=2.0, bias=log_floor[:, 0:1])

        def fin1(piece, ft):
            group, i = divmod(ft, GROUP)
            acc = product(1, piece, ft, psum_fin, "fin")
            if i == 0:
                neg_h_tiles[(piece, group)] = work.tile([P, GROUP, piece[1] * PAIRS], BF16, tag="neg_h", name="neg_h")
            nc.vector.scalar_tensor_tensor(
                out=neg_h_tiles[(piece, group)][:, i, :], in0=acc[:], scalar=bias["shift1"][:, ft : ft + 1],
                in1=sig_tiles[(1, piece, group)][:, i, :], op0=ALU.add, op1=ALU.min,
            )

        def lay(piece, group, engine, run, first, last):
            if (piece, group) not in h_tiles:
                h_tiles[(piece, group)] = work.tile(
                    [P, piece[1] * PAIRS, PACK], BF16, align_bytes=64, tag="h_grouped", name="h_grouped"
                )
            engine.tensor_scalar(
                out=h_tiles[(piece, group)][:, first:last, :].rearrange("p (c i) t -> p c t i", i=run),
                in0=neg_h_tiles[(piece, group)][:, :, first:last].rearrange("p t (c i) -> p c t i", i=run),
                scalar1=-1.0, scalar2=0.0, op0=ALU.mult, op1=ALU.add,
            )

        def quant_h(piece, group):
            tokens = span(piece)
            nc.vector.quantize_mx(
                out=h_codes[:, group, tokens].bitcast(FP8X4), scales=h_scales[:, group, tokens],
                in_=h_tiles[(piece, group)][:].rearrange("p w t -> p (w t)"),
            )

        def relu2(piece, ft):
            acc = accs[(piece, ft)]
            dst = excess[:, ft, 0 : piece[1] * PAIRS]
            if piece[0] == 0:
                nc.vector.tensor_scalar(
                    out=dst, in0=acc[:], scalar1=bias["lim2"][:, ft : ft + 1],
                    scalar2=bias["base2"][:, ft : ft + 1], op0=ALU.min, op1=ALU.add,
                )
            else:
                nc.vector.scalar_tensor_tensor(
                    out=dst, in0=acc[:], scalar=bias["lim2"][:, ft : ft + 1],
                    in1=dst, op0=ALU.min, op1=ALU.add,
                )

        def atom(piece, j, group):
            half, place = divmod(piece[0] + j, 4)
            dst = prods[:, half, group * GROUP : (group + 1) * GROUP, :]
            src = sig_tiles[(2, piece, group)][:, :, j * PAIRS : (j + 1) * PAIRS]
            if place == 0:
                nc.vector.tensor_scalar(out=dst, in0=src, scalar1=CLAMP, scalar2=None, op0=ALU.max)
            else:
                nc.vector.scalar_tensor_tensor(out=dst, in0=src, scalar=CLAMP, in1=dst, op0=ALU.max, op1=ALU.mult)

        def pair_product(piece, group):
            src = sig_tiles[(2, piece, group)]
            flat = src[:].rearrange("p i w -> p (i w)")
            nc.vector.tensor_scalar(out=flat, in0=flat, scalar1=CLAMP, scalar2=None, op0=ALU.max)
            nc.gpsimd.tensor_tensor(
                out=prods[:, piece[0] // 4, group * GROUP : (group + 1) * GROUP, :],
                in0=src[:, :, 0:PAIRS], in1=src[:, :, PAIRS : 2 * PAIRS], op=ALU.mult,
            )

        def fin2(piece, ft):
            group, i = divmod(ft, GROUP)
            acc = again[ft]
            part = sig_tiles[(2, piece, group)][:, i, :]
            nc.vector.scalar_tensor_tensor(
                out=part, in0=acc[:], scalar=bias["shift2"][:, ft : ft + 1], in1=part, op0=ALU.add, op1=ALU.min,
            )

        def log_prod(half, first, count):
            part = prods[:, half, first : first + count, :].rearrange("p f a -> p (f a)")
            nc.scalar.activation(out=part, in_=part, func=ACT.Ln, scale=PROD_SCALE)

        out_rows = out.rearrange("b i f -> (b i) f").rearrange("(p h) f -> p h f", h=2)

        turned = {}

        def turn_in(group, h, parts, first, last):
            if first:
                turned[(group, h)] = psum_sig.tile([P, GROUP, P], F32, tag="sig", name="turned")
            for n, (i, part) in enumerate(parts):
                nc.tensor.matmul(
                    out=turned[(group, h)][:, i, :], lhsT=part, rhs=ident[:], is_transpose=True,
                    start=(first and n == 0), stop=(last and n == len(parts) - 1),
                )

        def prod_parts(part, group, h, first=0, count=GROUP):
            return [(i, prods[:, part, group * GROUP + i, h * P : (h + 1) * P]) for i in range(first, first + count)]

        def excess_parts(group, h):
            return [
                (i, excess[:, group * GROUP + i, j * PAIRS + h * P : j * PAIRS + (h + 1) * P])
                for i in range(GROUP)
                for j in range(2)
            ]

        def last_parts(i, h):
            return [
                (i, sig_tiles[(2, SECOND[1], 1)][:, i, j * PAIRS + h * P : j * PAIRS + (h + 1) * P])
                for j in range(2)
            ]

        def store(group, h, parts=1):
            width = BANK // parts
            result = work.tile([P, BANK], F32, tag="result", name="result", bufs=4)
            for n in range(parts):
                here = slice(n * width, (n + 1) * width)
                cols = slice(group * BANK + n * width, group * BANK + (n + 1) * width)
                nc.vector.scalar_tensor_tensor(
                    out=result[:, here], in0=turned[(group, h)][:].rearrange("p i m -> p (i m)")[:, here], scalar=-1.0,
                    in1=x_sb[:, h, cols], op0=ALU.mult, op1=ALU.mult,
                )
                nc.sync.dma_start(out=out_rows[:, h, cols], in_=result[:, here])

        def finish(pieces, hooks):
            pending = None
            n = 0
            for piece in pieces:
                width = piece[1] * PAIRS
                for group in range(2):
                    for i in range(GROUP):
                        fin1(piece, group * GROUP + i)
                        n += 1
                        if n in hooks:
                            hooks[n]()
                        if i == 2 and pending is not None:
                            lay(*pending, nc.vector, 4, pending[0][1] * PAIRS // 2, pending[0][1] * PAIRS)
                        if i == 3 and pending is not None:
                            quant_h(*pending)
                    pending = (piece, group)
                    last = n == len(pieces) * FT
                    lay(piece, group, nc.gpsimd, 1, 0, width if last else width // 2)

        def logs(pieces):
            for n, piece in enumerate(pieces):
                logarithm(1, piece, 0, GROUP if n == 0 else 1)
                logarithm(1, piece, 1, 2 if n == 0 else 1)

        def sig1(piece, first=0, last=FT):
            for ft in range(first, last):
                sigmoid(1, piece, ft)

        def sig2(piece, group):
            for i in range(GROUP):
                sigmoid(2, piece, group * GROUP + i)

        def over2(piece, group):
            for i in range(GROUP):
                relu2(piece, group * GROUP + i)

        for piece in FIRST:
            sig1(piece)
        logs(FIRST)
        finish(FIRST, {4: lambda: sig1(SECOND[0], 0, 4)})
        sig1(SECOND[0], 4, FT)
        sig2(FIRST[0], 0)
        sig2(FIRST[0], 1)
        over2(FIRST[0], 0)
        quant_h(FIRST[1], 1)
        sig2(FIRST[1], 0)
        over2(FIRST[0], 1)
        sig2(FIRST[1], 1)
        over2(FIRST[1], 0)
        over2(FIRST[1], 1)
        sig1(SECOND[1])
        for piece in FIRST:
            for j in range(piece[1]):
                for group in range(2):
                    atom(piece, j, group)
        logs(SECOND)
        log_prod(0, 0, FT)
        finish(SECOND, {})
        sig2(SECOND[0], 0)
        sig2(SECOND[0], 1)
        over2(SECOND[0], 0)
        quant_h(SECOND[1], 1)
        sig2(SECOND[1], 0)
        relu2(SECOND[0], 4)
        relu2(SECOND[0], 5)
        pair_product(SECOND[0], 0)
        relu2(SECOND[0], 6)
        relu2(SECOND[0], 7)
        sig2(SECOND[1], 1)
        over2(SECOND[1], 0)
        last = SECOND[1]
        atom(last, 0, 0)
        atom(SECOND[0], 0, 1)
        logarithm(2, last, 1, GROUP)
        again = {}

        def repeat(ft):
            again[ft] = product(2, last, ft, psum_fin, "fin")

        repeat(GROUP)
        for group in range(2):
            for h in range(2):
                turn_in(group, h, prod_parts(0, group, h), True, False)
        repeat(GROUP + 1)
        fin2(last, GROUP)
        atom(last, 1, 0)
        log_prod(1, 0, GROUP)
        atom(SECOND[0], 1, 1)
        log_prod(1, GROUP, GROUP)
        for h in range(2):
            turn_in(0, h, excess_parts(0, h), False, False)
        repeat(GROUP + 2)
        for h in range(2):
            turn_in(1, h, excess_parts(1, h), False, False)
        repeat(GROUP + 3)
        for ft in range(GROUP + 1, FT):
            fin2(last, ft)
        for i in range(2):
            for h in range(2):
                turn_in(1, h, last_parts(i, h), False, False)
        for h in range(2):
            turn_in(0, h, prod_parts(1, 0, h), False, True)
        for i in range(2, GROUP):
            for h in range(2):
                turn_in(1, h, last_parts(i, h), False, False)
        for h in range(2):
            turn_in(1, h, prod_parts(1, 1, h), False, True)
        for h in range(2):
            store(0, h)
        store(1, 0)
        store(1, 1, 2)
